import numpy as np
import ml_dtypes


def mxq(x, axis, fmt="e4m3"):
    dtype, down = {"e4m3": (ml_dtypes.float8_e4m3fn, 7), "e5m2": (ml_dtypes.float8_e5m2, 14)}[fmt]
    v = np.moveaxis(np.asarray(x, np.float32).astype(ml_dtypes.bfloat16).astype(np.float64), axis, -1)
    blocks = v.reshape(v.shape[:-1] + (-1, 32))
    amax = np.abs(blocks).max(-1, keepdims=True)
    byte = np.maximum(np.where(amax > 0, np.frexp(amax)[1] - 1 + 127, 0) - down, 1)
    scale = np.exp2(byte - 127.0)
    codes = (blocks / scale).astype(np.float32).astype(dtype).astype(np.float64)
    return np.moveaxis((codes * scale).reshape(v.shape), -1, axis)


WIDE = False


def mx_kscale(k):
    if not WIDE:
        return np.ones(k)
    levels = np.array([10, -10, 5, -5, 0])
    a = np.random.permutation(np.resize(levels, k // 512 * 4)).reshape(k // 512, 4)
    idx = np.arange(k)
    return np.exp2(a[idx // 512, idx % 128 // 32])


BF16 = ml_dtypes.bfloat16


def bf(x):
    return np.asarray(x, np.float32).astype(BF16)


def f64(x):
    return np.asarray(x).astype(np.float64)


E2M1 = np.array([0.0, 0.5, 1.0, 1.5, 2.0, 3.0, 4.0, 6.0, -0.0, -0.5, -1.0, -1.5, -2.0, -3.0, -4.0, -6.0])


def pack_weight(w, fmt):
    k, n = w.shape
    w = f64(bf(w)).reshape(k // 32, 32, n)
    amax = np.abs(w).max(1)
    if fmt == "e4m3":
        byte = np.frexp(amax)[1] - 1 + 127 - 7
    else:
        mant, ex = np.frexp(amax / 6.0)
        byte = np.where(mant > 0.5, ex, ex - 1) + 127
    byte = np.clip(np.where(amax > 0, byte, 1), 1, 254)
    scaled = (w * np.exp2(127.0 - byte)[:, None, :]).reshape(k, n).astype(np.float32)
    by_word = np.ascontiguousarray(scaled.reshape(k // 512, 128, 4, n).transpose(0, 1, 3, 2))
    if fmt == "e4m3":
        words = by_word.astype(ml_dtypes.float8_e4m3fn).view(np.uint8)
    else:
        c = by_word.astype(ml_dtypes.float4_e2m1fn).view(np.uint8) & 0xF
        words = c[..., 0::2] | (c[..., 1::2] << 4)
    return np.ascontiguousarray(words), np.ascontiguousarray(byte.astype(np.uint8).reshape(k // 512, 16, n))


def unpack_weight(words, scales, fmt):
    g, p, n, _ = words.shape
    if fmt == "e4m3":
        vals = np.ascontiguousarray(words).view(ml_dtypes.float8_e4m3fn).astype(np.float64)
    else:
        nib = np.empty((g, p, n, 4), np.uint8)
        nib[..., 0::2] = words & 0xF
        nib[..., 1::2] = words >> 4
        vals = E2M1[nib]
    vals = vals * np.repeat(np.exp2(scales.astype(np.float64) - 127.0), 8, axis=1)[..., None]
    return vals.transpose(0, 1, 3, 2).reshape(g * 512, n)

def pack4(w):
    words, scales = pack_weight(w, "e2m1")
    return words.reshape(words.shape[0], 128, -1), scales


def unpack4(words, scales):
    return unpack_weight(words.reshape(words.shape[0], 128, -1, 2), scales, "e2m1")


B, DI, DH = 1024, 1024, 256


def sigmoid(v):
    return 1.0 / (1.0 + np.exp(-v))


def setup_inputs():
    s = mx_kscale(DI)
    n = np.random.standard_normal
    a, c = 0.7 / np.sqrt(DI), 0.7 / np.sqrt(DH)
    keep = np.random.uniform(size=B) < 0.9
    out = {
        "x": bf(n((B, DI)) * s),
        "h_minors": bf(n((B, DH))),
        "c_minors": bf(n((B, DH))),
        "s0": bf(n((B, DH))),
        "s1": bf(n((B, DH))),
        "s2": bf(n((B, DH))),
        "mask": bf(keep * (0.5 + 0.5 * np.random.uniform(size=B))),
    }
    words, scales = pack4((n((7 * DH, DI)) * a / s).T)
    out["weight_ih_words"] = words
    out["weight_ih_scales"] = scales
    out.update({
        "bias_ih": bf(n(7 * DH) * 0.3),
        "weight_hh": bf(n((4 * DH, DH)) * c),
        "bias_hh": bf(n(4 * DH) * 0.3),
        "weight_sh0": bf(n((DH, DH)) * c),
        "bias_sh0": bf(n(DH) * 0.3),
        "weight_sh1": bf(n((DH, DH)) * c),
        "bias_sh1": bf(n(DH) * 0.3),
        "weight_sh2": bf(n((DH, DH)) * c),
        "bias_sh2": bf(n(DH) * 0.3),
    })
    return out


def reference(x, h_minors, c_minors, s0, s1, s2, mask, weight_ih_words, weight_ih_scales, bias_ih, weight_hh, bias_hh,
              weight_sh0, bias_sh0, weight_sh1, bias_sh1, weight_sh2, bias_sh2):
    d = DH
    m = f64(mask)[:, None]

    tmp = (mxq(f64(x), 1, "e4m3") @ unpack4(weight_ih_words, weight_ih_scales)) + f64(bias_ih)
    tmp2 = f64(h_minors) @ f64(weight_hh).T + f64(bias_hh)
    tmp3 = np.concatenate([
        f64(s0) @ f64(weight_sh0).T + f64(bias_sh0),
        f64(s1) @ f64(weight_sh1).T + f64(bias_sh1),
        f64(s2) @ f64(weight_sh2).T + f64(bias_sh2),
    ], axis=1)

    tmp_in, tmp_s = tmp[:, :4 * d], tmp[:, 4 * d:]
    pre = tmp_in + tmp2
    ifo = sigmoid(pre[:, :3 * d])
    c_hat = pre[:, 3 * d:]
    i_g, f_g, o_g = ifo[:, :d], ifo[:, d:2 * d], ifo[:, 2 * d:]

    c_t = (f_g * f64(c_minors) + i_g * np.tanh(c_hat)) * m
    tc = np.tanh(c_t) * m
    h = o_g * tc

    bg = sigmoid(tmp_s + tmp3)
    b0, b1, b2 = bg[:, :d], bg[:, d:2 * d], bg[:, 2 * d:]

    s_0 = (b0 + 1.0 - o_g) * tc
    s_1 = (b1 + 2.0 - o_g - s_0) * 0.5 * tc
    s_2 = (b2 + 3.0 - o_g - (2.0 * s_0 + s_1)) * (1.0 / 3.0) * tc

    return (h, c_t, s_0, s_1, s_2)

@@ -1,0 +1,273 @@
+from contextlib import ExitStack
+
+import concourse.mybir as mybir
+from concourse.masks import make_identity
+
+F32 = mybir.dt.float32
+BF16 = mybir.dt.bfloat16
+I32 = mybir.dt.int32
+U32 = mybir.dt.uint32
+U8 = mybir.dt.uint8
+FP8X4 = mybir.dt.float8_e4m3fn_x4
+FP4X4 = mybir.dt.float4_e2m1fn_x4
+ALU = mybir.AluOpType
+ACT = mybir.ActivationFunctionType
+
+P = 128
+ROWS = 1024
+DI = 1024
+DH = 256
+TILES = ROWS // P
+PAIRS = TILES // 2
+LSTM = 4 * DH
+GATES = 7 * DH
+K_PASS = 4 * P
+PASSES = DI // K_PASS
+BANK = 512
+
+FLOPS = 2 * ROWS * GATES * (DI + DH)
+
+
+def tile_share_lstm_cell_pa_kernel(
+    tc,
+    x,
+    h_minors,
+    c_minors,
+    s0,
+    s1,
+    s2,
+    mask,
+    weight_ih_words,
+    weight_ih_scales,
+    bias_ih,
+    weight_hh,
+    bias_hh,
+    weight_sh0,
+    bias_sh0,
+    weight_sh1,
+    bias_sh1,
+    weight_sh2,
+    bias_sh2,
+    out_0,
+    out_1,
+    out_2,
+    out_3,
+    out_4,
+):
+    nc = tc.nc
+    with ExitStack() as ctx:
+        keep = ctx.enter_context(tc.tile_pool(name="keep", bufs=1))
+        stage = ctx.enter_context(tc.tile_pool(name="stage", bufs=3))
+        chain = ctx.enter_context(tc.tile_pool(name="chain", bufs=4))
+        temps = ctx.enter_context(tc.tile_pool(name="temps", bufs=2))
+        results = ctx.enter_context(tc.tile_pool(name="results", bufs=2))
+        psum_tr = ctx.enter_context(tc.psum_pool(name="psum_tr", bufs=2))
+        psum_plain = ctx.enter_context(tc.psum_pool(name="psum_plain", bufs=3))
+        psum_mx = ctx.enter_context(tc.psum_pool(name="psum_mx", bufs=3))
+
+        ident = keep.tile([P, P], F32)
+        make_identity(nc, ident[:])
+        ones = keep.tile([P, P], BF16)
+        nc.vector.memset(ones[:], 1.0)
+        w_scales = keep.tile([P, PASSES, GATES], U8, align_bytes=64)
+        nc.vector.memset(w_scales[:].rearrange("p g n -> p (g n)").bitcast(I32), 0)
+        bias_rows = keep.tile([P, GATES - LSTM], BF16)
+        nc.vector.memset(bias_rows[:], 0.0)
+
+        bias_ih_bc = keep.tile([P, LSTM], BF16)
+        nc.gpsimd.dma_start(out=bias_ih_bc[:], in_=bias_ih[0:LSTM].partition_broadcast(P))
+        bias_hh_bc = keep.tile([P, LSTM], BF16)
+        nc.gpsimd.dma_start(out=bias_hh_bc[:], in_=bias_hh.partition_broadcast(P))
+        nc.gpsimd.dma_start(out=bias_rows[0:1, :], in_=bias_ih[LSTM:GATES].unsqueeze(0))
+        for j, bias_sh in enumerate((bias_sh0, bias_sh1, bias_sh2)):
+            nc.gpsimd.dma_start(out=bias_rows[1:2, j * DH : (j + 1) * DH], in_=bias_sh.unsqueeze(0))
+        mask_bf = keep.tile([P, TILES], BF16)
+        nc.gpsimd.dma_start(out=mask_bf[:], in_=mask.rearrange("(p t) -> p t", t=TILES))
+        c_sb = keep.tile([P, TILES, DH], BF16)
+        nc.gpsimd.dma_start(out=c_sb[:], in_=c_minors.rearrange("(p t) d -> p t d", t=TILES))
+
+        whh_sb = keep.tile([P, LSTM // P, DH], BF16)
+        nc.sync.dma_start(out=whh_sb[:], in_=weight_hh.rearrange("(j p) k -> p j k", p=P))
+        weight_row_tiles = [whh_sb[:, j, :] for j in range(LSTM // P)]
+        for i, weight_sh in enumerate((weight_sh0, weight_sh1, weight_sh2)):
+            wsh_sb = keep.tile([P, DH // P, DH], BF16, name="wsh_sb%d" % i)
+            nc.sync.dma_start(out=wsh_sb[:], in_=weight_sh.rearrange("(j p) k -> p j k", p=P))
+            weight_row_tiles.extend([wsh_sb[:, j, :] for j in range(DH // P)])
+
+        x_sb = keep.tile([P, TILES, DI], BF16)
+        x_view = x.rearrange("(p t) k -> p t k", t=TILES)
+        state_views = [s.rearrange("(p t) d -> p t d", t=TILES) for s in (h_minors, s0, s1, s2)]
+        state_sb = [keep.tile([P, TILES, DH], BF16, name="state_sb%d" % j) for j in range(4)]
+
+        def load_pair(q):
+            two = slice(2 * q, 2 * q + 2)
+            for t in (2 * q, 2 * q + 1):
+                nc.sync.dma_start(out=x_sb[:, t, :], in_=x_view[:, t, :])
+            for j in range(4):
+                nc.sync.dma_start(out=state_sb[j][:, two, :], in_=state_views[j][:, two, :])
+
+        load_pair(0)
+        w_words = keep.tile([P, PASSES, 2 * GATES], U8, align_bytes=64)
+        for quad in range(4):
+            nc.sync.dma_start(
+                out=w_scales[32 * quad : 32 * quad + 4, :, :].bitcast(I32),
+                in_=weight_ih_scales[:, 4 * quad : 4 * quad + 4, :].bitcast(I32).rearrange("g r n -> r g n"),
+            )
+        for g in range(PASSES):
+            nc.sync.dma_start(out=w_words[:, g, :].bitcast(I32), in_=weight_ih_words[g].bitcast(I32))
+        for q in range(1, PAIRS):
+            load_pair(q)
+
+        mask_f = keep.tile([P, TILES], F32)
+        nc.vector.tensor_copy(out=mask_f[:], in_=mask_bf[:])
+        bias_lstm = keep.tile([P, LSTM], F32)
+        nc.vector.tensor_tensor(out=bias_lstm[:], in0=bias_ih_bc[:], in1=bias_hh_bc[:], op=ALU.add)
+
+        w_t = keep.tile([P, GATES], F32)
+        for first in range(0, len(weight_row_tiles), 4):
+            group = weight_row_tiles[first : first + 4]
+            wt_ps = psum_tr.tile([P, 4, P], F32, tag="tr")
+            for j, rows in enumerate(group):
+                nc.tensor.transpose(wt_ps[:, j, :], rows.bitcast(F32), ident[:])
+            nc.vector.tensor_copy(
+                out=w_t[:, first * P : (first + len(group)) * P],
+                in_=wt_ps[:, 0 : len(group), :].rearrange("p j n -> p (j n)"),
+            )
+        w_t_halves = w_t[:].bitcast(BF16).rearrange("p (n e) -> p n e", e=2)
+
+        x_codes = keep.tile([P, TILES, PASSES * P], U32, align_bytes=64)
+        x_scales = keep.tile([P, TILES, PASSES * P], U8, align_bytes=64)
+        states_t = {}
+        gates = {}
+
+        def transpose_tile(t):
+            x_words = x_sb[:, t, :].bitcast(F32)
+            xt_ps = psum_tr.tile([P, PASSES, 2, P], F32, tag="tr")
+            for g in range(PASSES):
+                for u in range(2):
+                    nc.tensor.transpose(
+                        xt_ps[:, g, u, :], x_words[:, (K_PASS // 2) * g + u : (K_PASS // 2) * (g + 1) : 2], ident[:]
+                    )
+            st_ps = psum_tr.tile([P, 4, P], F32, tag="tr")
+            for j in range(4):
+                nc.tensor.transpose(st_ps[:, j, :], state_sb[j][:, t, :].bitcast(F32), ident[:])
+            grouped = stage.tile([P, PASSES, P, 4], BF16, align_bytes=64)
+            nc.scalar.copy(out=grouped[:].bitcast(F32), in_=xt_ps[:].rearrange("p g u r -> p g r u"))
+            st_sb = stage.tile([P, 4, P], F32)
+            nc.scalar.copy(out=st_sb[:], in_=st_ps[:])
+            states_t[t] = st_sb[:].bitcast(BF16).rearrange("p j (r e) -> p j r e", e=2)
+            nc.vector.quantize_mx(
+                out=x_codes[:, t, :].bitcast(FP8X4),
+                scales=x_scales[:, t, :],
+                in_=grouped[:].rearrange("p g r k -> p (g r k)"),
+            )
+
+        def gate_sums(t):
+            pre = stage.tile([P, GATES], F32)
+            for c0 in range(0, GATES, BANK):
+                width = min(BANK, GATES - c0)
+                cols = slice(c0, c0 + width)
+                plain = psum_plain.tile([P, BANK], F32)
+                for b0 in range(c0, c0 + width, DH):
+                    source = max(0, b0 // DH - 3)
+                    group = plain[:, b0 - c0 : b0 - c0 + DH]
+                    if b0 >= LSTM:
+                        nc.tensor.matmul(
+                            group, lhsT=ones[:], rhs=bias_rows[:, b0 - LSTM : b0 - LSTM + DH], start=True, stop=False
+                        )
+                    for e in range(2):
+                        nc.tensor.matmul(
+                            group,
+                            lhsT=states_t[t][:, source, :, e],
+                            rhs=w_t_halves[:, b0 : b0 + DH, e],
+                            start=(e == 0 and b0 < LSTM),
+                            stop=(e == 1),
+                        )
+                acc = psum_mx.tile([P, BANK], F32)
+                step = BANK if width == BANK else P
+                for n0 in range(c0, c0 + width, step):
+                    for g in range(PASSES):
+                        nc.tensor.matmul_mx(
+                            out=acc[:, n0 - c0 : n0 - c0 + step],
+                            lhsT=x_codes[:, t, g * P : (g + 1) * P].bitcast(FP8X4),
+                            lhsT_scale=x_scales[:, t, g * P : (g + 1) * P],
+                            rhs=w_words[:, g, 2 * n0 : 2 * (n0 + step)].bitcast(FP4X4),
+                            rhs_scale=w_scales[:, g, n0 : n0 + step],
+                            start=(g == 0),
+                            stop=(g == PASSES - 1),
+                        )
+                if c0 < LSTM:
+                    nc.vector.tensor_tensor(out=pre[:, cols], in0=plain[:, 0:width], in1=bias_lstm[:, cols], op=ALU.add)
+                else:
+                    nc.scalar.copy(out=pre[:, cols], in_=plain[:, 0:width])
+                nc.vector.tensor_tensor(out=pre[:, cols], in0=acc[:, 0:width], in1=pre[:, cols], op=ALU.add)
+            gate = chain.tile([P, GATES], F32)
+            nc.scalar.activation(out=gate[:, 0 : 3 * DH], in_=pre[:, 0 : 3 * DH], func=ACT.Sigmoid)
+            nc.scalar.activation(out=gate[:, 3 * DH : LSTM], in_=pre[:, 3 * DH : LSTM], func=ACT.Tanh)
+            nc.scalar.activation(out=gate[:, LSTM:GATES], in_=pre[:, LSTM:GATES], func=ACT.Sigmoid)
+            gates[t] = gate
+
+        out_views = [o.rearrange("(p t) d -> p t d", t=TILES) for o in (out_0, out_1, out_2, out_3, out_4)]
+
+        def finish_pair(q):
+            pair = (2 * q, 2 * q + 1)
+            res = results.tile([P, 5, 2, DH], F32)
+            h_out, c_out, s0_out, s1_out, s2_out = [[res[:, k, n, :] for n in range(2)] for k in range(5)]
+            m = [mask_f[:, t : t + 1] for t in pair]
+            i_g = [gates[t][:, 0:DH] for t in pair]
+            f_g = [gates[t][:, DH : 2 * DH] for t in pair]
+            o_g = [gates[t][:, 2 * DH : 3 * DH] for t in pair]
+            c_hat = [gates[t][:, 3 * DH : LSTM] for t in pair]
+            b_g = [gates[t][:, LSTM:GATES].rearrange("p (j d) -> p j d", j=3) for t in pair]
+            both = range(2)
+
+            kept = [temps.tile([P, DH], F32, name="kept%d" % n) for n in both]
+            new = [temps.tile([P, DH], F32, name="new%d" % n) for n in both]
+            tanh_c = [temps.tile([P, DH], F32, name="tanh_c%d" % n) for n in both]
+            cell = [temps.tile([P, DH], F32, name="cell%d" % n) for n in both]
+            b_o = [temps.tile([P, 3, DH], F32, name="b_o%d" % n) for n in both]
+            rest1 = [temps.tile([P, DH], F32, name="rest1%d" % n) for n in both]
+            part2 = [temps.tile([P, DH], F32, name="part2%d" % n) for n in both]
+            rest2 = [temps.tile([P, DH], F32, name="rest2%d" % n) for n in both]
+
+            def fused(out, in0, scalar, in1, op0, op1):
+                nc.vector.scalar_tensor_tensor(out=out, in0=in0, scalar=scalar, in1=in1, op0=op0, op1=op1)
+
+            for n in both:
+                fused(kept[n][:], f_g[n], m[n], c_sb[:, pair[n], :], ALU.mult, ALU.mult)
+            for n in both:
+                fused(new[n][:], i_g[n], m[n], c_hat[n], ALU.mult, ALU.mult)
+            for n in both:
+                nc.vector.tensor_tensor(out=c_out[n], in0=kept[n][:], in1=new[n][:], op=ALU.add)
+            for n in both:
+                nc.scalar.activation(out=tanh_c[n][:], in_=c_out[n], func=ACT.Tanh)
+            for n in both:
+                nc.vector.tensor_tensor(
+                    out=b_o[n][:], in0=b_g[n], in1=o_g[n].unsqueeze(1).to_broadcast([P, 3, DH]), op=ALU.subtract
+                )
+            for n in both:
+                nc.scalar.activation(out=cell[n][:], in_=tanh_c[n][:], func=ACT.Copy, scale=m[n])
+            for n in both:
+                nc.vector.tensor_tensor(out=h_out[n], in0=o_g[n], in1=cell[n][:], op=ALU.mult)
+            for n in both:
+                fused(s0_out[n], b_o[n][:, 0, :], 1.0, cell[n][:], ALU.add, ALU.mult)
+            for n in both:
+                fused(rest1[n][:], b_o[n][:, 1, :], 2.0, s0_out[n], ALU.add, ALU.subtract)
+            for n in both:
+                fused(part2[n][:], s0_out[n], -2.0, b_o[n][:, 2, :], ALU.mult, ALU.add)
+            for n in both:
+                fused(s1_out[n], rest1[n][:], 0.5, cell[n][:], ALU.mult, ALU.mult)
+            for n in both:
+                fused(rest2[n][:], part2[n][:], 3.0, s1_out[n], ALU.add, ALU.subtract)
+            for n in both:
+                fused(s2_out[n], rest2[n][:], 1.0 / 3.0, cell[n][:], ALU.mult, ALU.mult)
+            for k in range(5):
+                nc.sync.dma_start(out=out_views[k][:, 2 * q : 2 * q + 2, :], in_=res[:, k, :, :])
+
+        transpose_tile(0)
+        for q in range(PAIRS):
+            for t in (2 * q, 2 * q + 1):
+                if t + 1 < TILES:
+                    transpose_tile(t + 1)
+                gate_sums(t)
+            finish_pair(q)

@@ -18,14 +18,19 @@ ROWS = 1024
 DI = 1024
 DH = 256
 TILES = ROWS // P
+HALVES = 2
+TILES_HALF = TILES // HALVES
 PAIRS = TILES // 2
 LSTM = 4 * DH
 GATES = 7 * DH
+GATE_TILES = GATES // P
 K_PASS = 4 * P
 PASSES = DI // K_PASS
 BANK = 512
 
 FLOPS = 2 * ROWS * GATES * (DI + DH)
+
+VECTOR_COPIES = ((1, 3, 5, 7, 9, 11, 13), (2, 5, 8, 11))
 
 
 def tile_share_lstm_cell_pa_kernel(
@@ -59,33 +64,61 @@ def tile_share_lstm_cell_pa_kernel(
         keep = ctx.enter_context(tc.tile_pool(name="keep", bufs=1))
         stage = ctx.enter_context(tc.tile_pool(name="stage", bufs=3))
         chain = ctx.enter_context(tc.tile_pool(name="chain", bufs=4))
-        temps = ctx.enter_context(tc.tile_pool(name="temps", bufs=2))
+        temps = ctx.enter_context(tc.tile_pool(name="temps", bufs=1))
         results = ctx.enter_context(tc.tile_pool(name="results", bufs=2))
         psum_tr = ctx.enter_context(tc.psum_pool(name="psum_tr", bufs=2))
-        psum_plain = ctx.enter_context(tc.psum_pool(name="psum_plain", bufs=3))
-        psum_mx = ctx.enter_context(tc.psum_pool(name="psum_mx", bufs=3))
+        psum_sum = ctx.enter_context(tc.psum_pool(name="psum_sum", bufs=6))
 
         ident = keep.tile([P, P], F32)
         make_identity(nc, ident[:])
-        ones = keep.tile([P, P], BF16)
-        nc.vector.memset(ones[:], 1.0)
+        warm_in = keep.tile([P, 1], F32)
+        nc.vector.memset(warm_in[:], 0.0)
+        warm_out = keep.tile([P, 1], F32)
+        nc.scalar.activation(out=warm_out[:], in_=warm_in[:], func=ACT.Sigmoid)
         w_scales = keep.tile([P, PASSES, GATES], U8, align_bytes=64)
         nc.vector.memset(w_scales[:].rearrange("p g n -> p (g n)").bitcast(I32), 0)
-        bias_rows = keep.tile([P, GATES - LSTM], BF16)
-        nc.vector.memset(bias_rows[:], 0.0)
+        bias_x_rows = keep.tile([P, P], BF16)
+        nc.vector.memset(bias_x_rows[:], 0.0)
+        bias_s_rows = keep.tile([P, P], BF16)
+        nc.vector.memset(bias_s_rows[:], 0.0)
 
-        bias_ih_bc = keep.tile([P, LSTM], BF16)
-        nc.gpsimd.dma_start(out=bias_ih_bc[:], in_=bias_ih[0:LSTM].partition_broadcast(P))
-        bias_hh_bc = keep.tile([P, LSTM], BF16)
-        nc.gpsimd.dma_start(out=bias_hh_bc[:], in_=bias_hh.partition_broadcast(P))
-        nc.gpsimd.dma_start(out=bias_rows[0:1, :], in_=bias_ih[LSTM:GATES].unsqueeze(0))
-        for j, bias_sh in enumerate((bias_sh0, bias_sh1, bias_sh2)):
-            nc.gpsimd.dma_start(out=bias_rows[1:2, j * DH : (j + 1) * DH], in_=bias_sh.unsqueeze(0))
+        nc.scalar.dma_start(out=bias_x_rows[0:GATE_TILES, :], in_=bias_ih.rearrange("(j p) -> j p", p=P))
+        nc.scalar.dma_start(out=bias_s_rows[0 : LSTM // P, :], in_=bias_hh.rearrange("(j p) -> j p", p=P))
+        for i, bias_sh in enumerate((bias_sh0, bias_sh1, bias_sh2)):
+            first = (LSTM + i * DH) // P
+            nc.scalar.dma_start(
+                out=bias_s_rows[first : first + DH // P, :], in_=bias_sh.rearrange("(j p) -> j p", p=P)
+            )
         mask_bf = keep.tile([P, TILES], BF16)
-        nc.gpsimd.dma_start(out=mask_bf[:], in_=mask.rearrange("(p t) -> p t", t=TILES))
+        nc.scalar.dma_start(out=mask_bf[:], in_=mask.rearrange("(p t) -> p t", t=TILES))
         c_sb = keep.tile([P, TILES, DH], BF16)
         nc.gpsimd.dma_start(out=c_sb[:], in_=c_minors.rearrange("(p t) d -> p t d", t=TILES))
 
+        x_sb = keep.tile([P, TILES, DI], BF16)
+        x_view = x.rearrange("(p t) k -> p t k", t=TILES)
+        state_views = [s.rearrange("(p t) d -> p t d", t=TILES) for s in (h_minors, s0, s1, s2)]
+        state_sb = [keep.tile([P, TILES, DH], BF16, name="state_sb%d" % j) for j in range(4)]
+
+        def load_x(half):
+            for t in range(half * TILES_HALF, (half + 1) * TILES_HALF):
+                nc.sync.dma_start(out=x_sb[:, t, :], in_=x_view[:, t, :])
+
+        def load_states(half):
+            four = slice(half * TILES_HALF, (half + 1) * TILES_HALF)
+            for j in range(4):
+                nc.sync.dma_start(out=state_sb[j][:, four, :], in_=state_views[j][:, four, :])
+
+        load_x(0)
+        w_words = keep.tile([P, PASSES, 2 * GATES], U8, align_bytes=64)
+        for quad in range(4):
+            nc.sync.dma_start(
+                out=w_scales[32 * quad : 32 * quad + 4, :, :].bitcast(I32),
+                in_=weight_ih_scales[:, 4 * quad : 4 * quad + 4, :].bitcast(I32).rearrange("g r n -> r g n"),
+            )
+        for part in range(2):
+            some = slice(part * GATES, (part + 1) * GATES)
+            for g in range(PASSES):
+                nc.sync.dma_start(out=w_words[:, g, some].bitcast(I32), in_=weight_ih_words[g][:, some].bitcast(I32))
         whh_sb = keep.tile([P, LSTM // P, DH], BF16)
         nc.sync.dma_start(out=whh_sb[:], in_=weight_hh.rearrange("(j p) k -> p j k", p=P))
         weight_row_tiles = [whh_sb[:, j, :] for j in range(LSTM // P)]
@@ -93,54 +126,43 @@ def tile_share_lstm_cell_pa_kernel(
             wsh_sb = keep.tile([P, DH // P, DH], BF16, name="wsh_sb%d" % i)
             nc.sync.dma_start(out=wsh_sb[:], in_=weight_sh.rearrange("(j p) k -> p j k", p=P))
             weight_row_tiles.extend([wsh_sb[:, j, :] for j in range(DH // P)])
-
-        x_sb = keep.tile([P, TILES, DI], BF16)
-        x_view = x.rearrange("(p t) k -> p t k", t=TILES)
-        state_views = [s.rearrange("(p t) d -> p t d", t=TILES) for s in (h_minors, s0, s1, s2)]
-        state_sb = [keep.tile([P, TILES, DH], BF16, name="state_sb%d" % j) for j in range(4)]
-
-        def load_pair(q):
-            two = slice(2 * q, 2 * q + 2)
-            for t in (2 * q, 2 * q + 1):
-                nc.sync.dma_start(out=x_sb[:, t, :], in_=x_view[:, t, :])
-            for j in range(4):
-                nc.sync.dma_start(out=state_sb[j][:, two, :], in_=state_views[j][:, two, :])
-
-        load_pair(0)
-        w_words = keep.tile([P, PASSES, 2 * GATES], U8, align_bytes=64)
-        for quad in range(4):
-            nc.sync.dma_start(
-                out=w_scales[32 * quad : 32 * quad + 4, :, :].bitcast(I32),
-                in_=weight_ih_scales[:, 4 * quad : 4 * quad + 4, :].bitcast(I32).rearrange("g r n -> r g n"),
-            )
-        for g in range(PASSES):
-            nc.sync.dma_start(out=w_words[:, g, :].bitcast(I32), in_=weight_ih_words[g].bitcast(I32))
-        for q in range(1, PAIRS):
-            load_pair(q)
+        load_states(0)
+        load_x(1)
+        load_states(1)
 
         mask_f = keep.tile([P, TILES], F32)
         nc.vector.tensor_copy(out=mask_f[:], in_=mask_bf[:])
-        bias_lstm = keep.tile([P, LSTM], F32)
-        nc.vector.tensor_tensor(out=bias_lstm[:], in0=bias_ih_bc[:], in1=bias_hh_bc[:], op=ALU.add)
+        bias_rows = keep.tile([P, P], F32)
+        nc.vector.tensor_tensor(out=bias_rows[:], in0=bias_x_rows[:], in1=bias_s_rows[:], op=ALU.add)
+        bias_col = keep.tile([P, GATE_TILES], F32)
+
+        def transpose_bias():
+            bias_ps = psum_tr.tile([P, 4, P], F32, tag="tr")
+            nc.tensor.transpose(bias_ps[:, 0, :], bias_rows[:], ident[:])
+            nc.vector.tensor_copy(out=bias_col[:], in_=bias_ps[:, 0, 0:GATE_TILES])
 
         w_t = keep.tile([P, GATES], F32)
-        for first in range(0, len(weight_row_tiles), 4):
-            group = weight_row_tiles[first : first + 4]
-            wt_ps = psum_tr.tile([P, 4, P], F32, tag="tr")
-            for j, rows in enumerate(group):
-                nc.tensor.transpose(wt_ps[:, j, :], rows.bitcast(F32), ident[:])
-            nc.vector.tensor_copy(
-                out=w_t[:, first * P : (first + len(group)) * P],
-                in_=wt_ps[:, 0 : len(group), :].rearrange("p j n -> p (j n)"),
-            )
         w_t_halves = w_t[:].bitcast(BF16).rearrange("p (n e) -> p n e", e=2)
 
-        x_codes = keep.tile([P, TILES, PASSES * P], U32, align_bytes=64)
-        x_scales = keep.tile([P, TILES, PASSES * P], U8, align_bytes=64)
-        states_t = {}
+        def transpose_weights():
+            for first in range(0, len(weight_row_tiles), 4):
+                group = weight_row_tiles[first : first + 4]
+                wt_ps = psum_tr.tile([P, 4, P], F32, tag="tr")
+                for j, rows in enumerate(group):
+                    nc.tensor.transpose(wt_ps[:, j, :], rows.bitcast(F32), ident[:])
+                nc.vector.tensor_copy(
+                    out=w_t[:, first * P : (first + len(group)) * P],
+                    in_=wt_ps[:, 0 : len(group), :].rearrange("p j n -> p (j n)"),
+                )
+
+        x_codes = keep.tile([P, HALVES, PASSES, TILES_HALF * P], U32, align_bytes=64)
+        x_scales = keep.tile([P, HALVES, PASSES, TILES_HALF * P], U8, align_bytes=64)
+        states_t_sb = keep.tile([P, TILES, 4, P], F32)
+        mx_sb = keep.tile([P, HALVES, GATE_TILES, BANK], F32)
         gates = {}
 
-        def transpose_tile(t):
+        def transpose_x(t):
+            half, place = divmod(t, TILES_HALF)
             x_words = x_sb[:, t, :].bitcast(F32)
             xt_ps = psum_tr.tile([P, PASSES, 2, P], F32, tag="tr")
             for g in range(PASSES):
@@ -148,63 +170,73 @@ def tile_share_lstm_cell_pa_kernel(
                     nc.tensor.transpose(
                         xt_ps[:, g, u, :], x_words[:, (K_PASS // 2) * g + u : (K_PASS // 2) * (g + 1) : 2], ident[:]
                     )
+            grouped = stage.tile([P, PASSES, P, 4], BF16, align_bytes=64)
+            nc.scalar.copy(out=grouped[:].bitcast(F32), in_=xt_ps[:].rearrange("p g u r -> p g r u"))
+            for g in range(PASSES):
+                nc.vector.quantize_mx(
+                    out=x_codes[:, half, g, place * P : (place + 1) * P].bitcast(FP8X4),
+                    scales=x_scales[:, half, g, place * P : (place + 1) * P],
+                    in_=grouped[:, g, :, :].rearrange("p r k -> p (r k)"),
+                )
+
+        def transpose_states(t):
             st_ps = psum_tr.tile([P, 4, P], F32, tag="tr")
             for j in range(4):
                 nc.tensor.transpose(st_ps[:, j, :], state_sb[j][:, t, :].bitcast(F32), ident[:])
-            grouped = stage.tile([P, PASSES, P, 4], BF16, align_bytes=64)
-            nc.scalar.copy(out=grouped[:].bitcast(F32), in_=xt_ps[:].rearrange("p g u r -> p g r u"))
-            st_sb = stage.tile([P, 4, P], F32)
-            nc.scalar.copy(out=st_sb[:], in_=st_ps[:])
-            states_t[t] = st_sb[:].bitcast(BF16).rearrange("p j (r e) -> p j r e", e=2)
-            nc.vector.quantize_mx(
-                out=x_codes[:, t, :].bitcast(FP8X4),
-                scales=x_scales[:, t, :],
-                in_=grouped[:].rearrange("p g r k -> p (g r k)"),
-            )
+            nc.scalar.copy(out=states_t_sb[:, t, :, :], in_=st_ps[:])
+
+        def mx_product(half, j):
+            acc = psum_sum.tile([P, BANK], F32, tag="bank")
+            for g in range(PASSES):
+                nc.tensor.matmul_mx(
+                    out=acc[:],
+                    lhsT=w_words[:, g, 2 * P * j : 2 * P * (j + 1)].bitcast(FP4X4),
+                    lhsT_scale=w_scales[:, g, P * j : P * (j + 1)],
+                    rhs=x_codes[:, half, g, :].bitcast(FP8X4),
+                    rhs_scale=x_scales[:, half, g, :],
+                    start=(g == 0),
+                    stop=(g == PASSES - 1),
+                )
+            if j in VECTOR_COPIES[half]:
+                nc.vector.tensor_scalar(
+                    out=mx_sb[:, half, j, :], in0=acc[:], scalar1=bias_col[:, j : j + 1], scalar2=None, op0=ALU.add
+                )
+            else:
+                nc.scalar.activation(out=mx_sb[:, half, j, :], in_=acc[:], func=ACT.Identity, bias=bias_col[:, j : j + 1])
 
         def gate_sums(t):
-            pre = stage.tile([P, GATES], F32)
+            half, place = divmod(t, TILES_HALF)
+            states_t = states_t_sb[:, t, :, :].bitcast(BF16).rearrange("p j (r e) -> p j r e", e=2)
+            gate = chain.tile([P, GATES], F32)
             for c0 in range(0, GATES, BANK):
                 width = min(BANK, GATES - c0)
-                cols = slice(c0, c0 + width)
-                plain = psum_plain.tile([P, BANK], F32)
-                for b0 in range(c0, c0 + width, DH):
+                total = psum_sum.tile([P, BANK], F32, tag="bank")
+                step = BANK if c0 < LSTM else DH
+                for b0 in range(c0, c0 + width, step):
                     source = max(0, b0 // DH - 3)
-                    group = plain[:, b0 - c0 : b0 - c0 + DH]
-                    if b0 >= LSTM:
-                        nc.tensor.matmul(
-                            group, lhsT=ones[:], rhs=bias_rows[:, b0 - LSTM : b0 - LSTM + DH], start=True, stop=False
-                        )
                     for e in range(2):
                         nc.tensor.matmul(
-                            group,
-                            lhsT=states_t[t][:, source, :, e],
-                            rhs=w_t_halves[:, b0 : b0 + DH, e],
-                            start=(e == 0 and b0 < LSTM),
-                            stop=(e == 1),
+                            total[:, b0 - c0 : b0 - c0 + step],
+                            lhsT=states_t[:, source, :, e],
+                            rhs=w_t_halves[:, b0 : b0 + step, e],
+                            start=(e == 0),
+                            stop=False,
                         )
-                acc = psum_mx.tile([P, BANK], F32)
-                step = BANK if width == BANK else P
-                for n0 in range(c0, c0 + width, step):
-                    for g in range(PASSES):
-                        nc.tensor.matmul_mx(
-                            out=acc[:, n0 - c0 : n0 - c0 + step],
-                            lhsT=x_codes[:, t, g * P : (g + 1) * P].bitcast(FP8X4),
-                            lhsT_scale=x_scales[:, t, g * P : (g + 1) * P],
-                            rhs=w_words[:, g, 2 * n0 : 2 * (n0 + step)].bitcast(FP4X4),
-                            rhs_scale=w_scales[:, g, n0 : n0 + step],
-                            start=(g == 0),
-                            stop=(g == PASSES - 1),
+                    blocks = range(b0 // P, (b0 + step) // P)
+                    for j in blocks:
+                        nc.tensor.matmul(
+                            total[:, j * P - c0 : (j + 1) * P - c0],
+                            lhsT=mx_sb[:, half, j, place * P : (place + 1) * P],
+                            rhs=ident[:],
+                            is_transpose=True,
+                            start=False,
+                            stop=(j == blocks[-1]),
                         )
-                if c0 < LSTM:
-                    nc.vector.tensor_tensor(out=pre[:, cols], in0=plain[:, 0:width], in1=bias_lstm[:, cols], op=ALU.add)
+                if c0 == 2 * DH:
+                    nc.scalar.activation(out=gate[:, c0 : c0 + DH], in_=total[:, 0:DH], func=ACT.Sigmoid)
+                    nc.scalar.activation(out=gate[:, c0 + DH : c0 + BANK], in_=total[:, DH:BANK], func=ACT.Tanh)
                 else:
-                    nc.scalar.copy(out=pre[:, cols], in_=plain[:, 0:width])
-                nc.vector.tensor_tensor(out=pre[:, cols], in0=acc[:, 0:width], in1=pre[:, cols], op=ALU.add)
-            gate = chain.tile([P, GATES], F32)
-            nc.scalar.activation(out=gate[:, 0 : 3 * DH], in_=pre[:, 0 : 3 * DH], func=ACT.Sigmoid)
-            nc.scalar.activation(out=gate[:, 3 * DH : LSTM], in_=pre[:, 3 * DH : LSTM], func=ACT.Tanh)
-            nc.scalar.activation(out=gate[:, LSTM:GATES], in_=pre[:, LSTM:GATES], func=ACT.Sigmoid)
+                    nc.scalar.activation(out=gate[:, c0 : c0 + width], in_=total[:, 0:width], func=ACT.Sigmoid)
             gates[t] = gate
 
         out_views = [o.rearrange("(p t) d -> p t d", t=TILES) for o in (out_0, out_1, out_2, out_3, out_4)]
@@ -264,10 +296,35 @@ def tile_share_lstm_cell_pa_kernel(
             for k in range(5):
                 nc.sync.dma_start(out=out_views[k][:, 2 * q : 2 * q + 2, :], in_=res[:, k, :, :])
 
-        transpose_tile(0)
-        for q in range(PAIRS):
-            for t in (2 * q, 2 * q + 1):
-                if t + 1 < TILES:
-                    transpose_tile(t + 1)
-                gate_sums(t)
-            finish_pair(q)
+        for t in range(TILES_HALF):
+            transpose_x(t)
+        transpose_bias()
+        for j in range(GATE_TILES):
+            mx_product(0, j)
+        transpose_weights()
+        transpose_states(0)
+        transpose_states(1)
+        gate_sums(0)
+        transpose_x(4)
+        transpose_states(2)
+        gate_sums(1)
+        finish_pair(0)
+        transpose_x(5)
+        transpose_states(3)
+        gate_sums(2)
+        transpose_x(6)
+        transpose_x(7)
+        gate_sums(3)
+        finish_pair(1)
+        transpose_states(4)
+        transpose_states(5)
+        for j in range(GATE_TILES):
+            mx_product(1, j)
+        gate_sums(4)
+        transpose_states(6)
+        gate_sums(5)
+        finish_pair(2)
+        transpose_states(7)
+        gate_sums(6)
+        gate_sums(7)
+        finish_pair(3)

@@ -20,7 +20,6 @@ DH = 256
 TILES = ROWS // P
 HALVES = 2
 TILES_HALF = TILES // HALVES
-PAIRS = TILES // 2
 LSTM = 4 * DH
 GATES = 7 * DH
 GATE_TILES = GATES // P
@@ -30,7 +29,7 @@ BANK = 512
 
 FLOPS = 2 * ROWS * GATES * (DI + DH)
 
-VECTOR_COPIES = ((1, 3, 5, 7, 9, 11, 13), (2, 5, 8, 11))
+VECTOR_COPIES = ((1, 3, 5, 7, 9, 11, 13), (0, 1, 2, 4, 5, 6, 8, 9, 10, 12, 13))
 
 
 def tile_share_lstm_cell_pa_kernel(
@@ -64,8 +63,8 @@ def tile_share_lstm_cell_pa_kernel(
         keep = ctx.enter_context(tc.tile_pool(name="keep", bufs=1))
         stage = ctx.enter_context(tc.tile_pool(name="stage", bufs=3))
         chain = ctx.enter_context(tc.tile_pool(name="chain", bufs=4))
-        temps = ctx.enter_context(tc.tile_pool(name="temps", bufs=1))
-        results = ctx.enter_context(tc.tile_pool(name="results", bufs=2))
+        temps = ctx.enter_context(tc.tile_pool(name="temps", bufs=2))
+        results = ctx.enter_context(tc.tile_pool(name="results", bufs=3))
         psum_tr = ctx.enter_context(tc.psum_pool(name="psum_tr", bufs=2))
         psum_sum = ctx.enter_context(tc.psum_pool(name="psum_sum", bufs=6))
 
@@ -241,60 +240,97 @@ def tile_share_lstm_cell_pa_kernel(
 
         out_views = [o.rearrange("(p t) d -> p t d", t=TILES) for o in (out_0, out_1, out_2, out_3, out_4)]
 
-        def finish_pair(q):
-            pair = (2 * q, 2 * q + 1)
-            res = results.tile([P, 5, 2, DH], F32)
-            h_out, c_out, s0_out, s1_out, s2_out = [[res[:, k, n, :] for n in range(2)] for k in range(5)]
-            m = [mask_f[:, t : t + 1] for t in pair]
-            i_g = [gates[t][:, 0:DH] for t in pair]
-            f_g = [gates[t][:, DH : 2 * DH] for t in pair]
-            o_g = [gates[t][:, 2 * DH : 3 * DH] for t in pair]
-            c_hat = [gates[t][:, 3 * DH : LSTM] for t in pair]
-            b_g = [gates[t][:, LSTM:GATES].rearrange("p (j d) -> p j d", j=3) for t in pair]
-            both = range(2)
+        def fused(out, in0, scalar, in1, op0, op1):
+            nc.vector.scalar_tensor_tensor(out=out, in0=in0, scalar=scalar, in1=in1, op0=op0, op1=op1)
 
-            kept = [temps.tile([P, DH], F32, name="kept%d" % n) for n in both]
-            new = [temps.tile([P, DH], F32, name="new%d" % n) for n in both]
-            tanh_c = [temps.tile([P, DH], F32, name="tanh_c%d" % n) for n in both]
-            cell = [temps.tile([P, DH], F32, name="cell%d" % n) for n in both]
-            b_o = [temps.tile([P, 3, DH], F32, name="b_o%d" % n) for n in both]
-            rest1 = [temps.tile([P, DH], F32, name="rest1%d" % n) for n in both]
-            part2 = [temps.tile([P, DH], F32, name="part2%d" % n) for n in both]
-            rest2 = [temps.tile([P, DH], F32, name="rest2%d" % n) for n in both]
+        work = {}
 
-            def fused(out, in0, scalar, in1, op0, op1):
-                nc.vector.scalar_tensor_tensor(out=out, in0=in0, scalar=scalar, in1=in1, op0=op0, op1=op1)
+        def cell_steps(t):
+            gate = gates[t]
+            m = mask_f[:, t : t + 1]
+            res = results.tile([P, 5, DH], F32)
+            kept = temps.tile([P, DH], F32)
+            new = temps.tile([P, DH], F32)
+            tanh_c = temps.tile([P, DH], F32)
+            cell = temps.tile([P, DH], F32)
+            b_o = temps.tile([P, 3, DH], F32)
+            work[t] = (res, cell, b_o)
+            o_g = gate[:, 2 * DH : 3 * DH]
+            b_g = gate[:, LSTM:GATES].rearrange("p (j d) -> p j d", j=3)
 
-            for n in both:
-                fused(kept[n][:], f_g[n], m[n], c_sb[:, pair[n], :], ALU.mult, ALU.mult)
-            for n in both:
-                fused(new[n][:], i_g[n], m[n], c_hat[n], ALU.mult, ALU.mult)
-            for n in both:
-                nc.vector.tensor_tensor(out=c_out[n], in0=kept[n][:], in1=new[n][:], op=ALU.add)
-            for n in both:
-                nc.scalar.activation(out=tanh_c[n][:], in_=c_out[n], func=ACT.Tanh)
-            for n in both:
+            def step_kept():
+                fused(kept[:], gate[:, DH : 2 * DH], m, c_sb[:, t, :], ALU.mult, ALU.mult)
+
+            def step_new():
+                fused(new[:], gate[:, 0:DH], m, gate[:, 3 * DH : LSTM], ALU.mult, ALU.mult)
+
+            def step_c():
+                nc.vector.tensor_tensor(out=res[:, 1, :], in0=kept[:], in1=new[:], op=ALU.add)
+                nc.scalar.activation(out=tanh_c[:], in_=res[:, 1, :], func=ACT.Tanh)
+                nc.scalar.activation(out=cell[:], in_=tanh_c[:], func=ACT.Copy, scale=m)
+                nc.sync.dma_start(out=out_views[1][:, t, :], in_=res[:, 1, :])
+
+            def step_b01():
                 nc.vector.tensor_tensor(
-                    out=b_o[n][:], in0=b_g[n], in1=o_g[n].unsqueeze(1).to_broadcast([P, 3, DH]), op=ALU.subtract
+                    out=b_o[:, 0:2, :], in0=b_g[:, 0:2, :], in1=o_g.unsqueeze(1).to_broadcast([P, 2, DH]), op=ALU.subtract
                 )
-            for n in both:
-                nc.scalar.activation(out=cell[n][:], in_=tanh_c[n][:], func=ACT.Copy, scale=m[n])
-            for n in both:
-                nc.vector.tensor_tensor(out=h_out[n], in0=o_g[n], in1=cell[n][:], op=ALU.mult)
-            for n in both:
-                fused(s0_out[n], b_o[n][:, 0, :], 1.0, cell[n][:], ALU.add, ALU.mult)
-            for n in both:
-                fused(rest1[n][:], b_o[n][:, 1, :], 2.0, s0_out[n], ALU.add, ALU.subtract)
-            for n in both:
-                fused(part2[n][:], s0_out[n], -2.0, b_o[n][:, 2, :], ALU.mult, ALU.add)
-            for n in both:
-                fused(s1_out[n], rest1[n][:], 0.5, cell[n][:], ALU.mult, ALU.mult)
-            for n in both:
-                fused(rest2[n][:], part2[n][:], 3.0, s1_out[n], ALU.add, ALU.subtract)
-            for n in both:
-                fused(s2_out[n], rest2[n][:], 1.0 / 3.0, cell[n][:], ALU.mult, ALU.mult)
-            for k in range(5):
-                nc.sync.dma_start(out=out_views[k][:, 2 * q : 2 * q + 2, :], in_=res[:, k, :, :])
+
+            def step_b2():
+                nc.vector.tensor_tensor(out=b_o[:, 2, :], in0=b_g[:, 2, :], in1=o_g, op=ALU.subtract)
+
+            return [step_kept, step_new, step_c, step_b01, step_b2]
+
+        def share_steps(t):
+            res, cell, b_o = work[t]
+            o_g = gates[t][:, 2 * DH : 3 * DH]
+            rest1 = temps.tile([P, DH], F32)
+            part2 = temps.tile([P, DH], F32)
+            rest2 = temps.tile([P, DH], F32)
+
+            def store(k):
+                nc.sync.dma_start(out=out_views[k][:, t, :], in_=res[:, k, :])
+
+            def step_s0():
+                fused(res[:, 2, :], b_o[:, 0, :], 1.0, cell[:], ALU.add, ALU.mult)
+                store(2)
+
+            def step_rest1():
+                fused(rest1[:], b_o[:, 1, :], 2.0, res[:, 2, :], ALU.add, ALU.subtract)
+
+            def step_s1():
+                fused(res[:, 3, :], rest1[:], 0.5, cell[:], ALU.mult, ALU.mult)
+                store(3)
+
+            def step_part2():
+                fused(part2[:], res[:, 2, :], -2.0, b_o[:, 2, :], ALU.mult, ALU.add)
+
+            def step_rest2():
+                fused(rest2[:], part2[:], 3.0, res[:, 3, :], ALU.add, ALU.subtract)
+
+            def step_s2():
+                fused(res[:, 4, :], rest2[:], 1.0 / 3.0, cell[:], ALU.mult, ALU.mult)
+                store(4)
+
+            def step_h():
+                nc.vector.tensor_tensor(out=res[:, 0, :], in0=o_g, in1=cell[:], op=ALU.mult)
+                store(0)
+
+            return [step_s0, step_rest1, step_s1, step_part2, step_rest2, step_s2, step_h]
+
+        def finish(t):
+            first = cell_steps(t) if t < TILES else []
+            second = share_steps(t - 1) if t > 0 else []
+            if not second:
+                order = first
+            elif not first:
+                s_0, r_1, s_1, p_2, r_2, s_2, h_t = second
+                order = [s_0, h_t, r_1, p_2, s_1, r_2, s_2]
+            else:
+                kept, new, c_t, b01, b_2 = first
+                s_0, r_1, s_1, p_2, r_2, s_2, h_t = second
+                order = [s_0, kept, r_1, new, s_1, p_2, c_t, r_2, b01, s_2, h_t, b_2]
+            for step in order:
+                step()
 
         for t in range(TILES_HALF):
             transpose_x(t)
@@ -305,26 +341,31 @@ def tile_share_lstm_cell_pa_kernel(
         transpose_states(0)
         transpose_states(1)
         gate_sums(0)
+        finish(0)
         transpose_x(4)
         transpose_states(2)
         gate_sums(1)
-        finish_pair(0)
+        finish(1)
         transpose_x(5)
         transpose_states(3)
         gate_sums(2)
+        finish(2)
         transpose_x(6)
         transpose_x(7)
         gate_sums(3)
-        finish_pair(1)
+        finish(3)
         transpose_states(4)
         transpose_states(5)
         for j in range(GATE_TILES):
             mx_product(1, j)
         gate_sums(4)
+        finish(4)
         transpose_states(6)
         gate_sums(5)
-        finish_pair(2)
+        finish(5)
         transpose_states(7)
         gate_sums(6)
+        finish(6)
         gate_sums(7)
-        finish_pair(3)
+        finish(7)
+        finish(8)

@@ -332,14 +332,17 @@ def tile_share_lstm_cell_pa_kernel(
             for step in order:
                 step()
 
+        ctx.enter_context(tc.manual_schedule(engines={mybir.EngineType.PE}))
         for t in range(TILES_HALF):
             transpose_x(t)
         transpose_bias()
         for j in range(GATE_TILES):
             mx_product(0, j)
-        transpose_weights()
-        transpose_states(0)
-        transpose_states(1)
+            if j == 6:
+                transpose_weights()
+            if j == 10:
+                transpose_states(0)
+                transpose_states(1)
         gate_sums(0)
         finish(0)
         transpose_x(4)

@@ -146,7 +146,7 @@ def tile_share_lstm_cell_pa_kernel(
         def transpose_weights():
             for first in range(0, len(weight_row_tiles), 4):
                 group = weight_row_tiles[first : first + 4]
-                wt_ps = psum_tr.tile([P, 4, P], F32, tag="tr")
+                wt_ps = psum_sum.tile([P, 4, P], F32, tag="bank")
                 for j, rows in enumerate(group):
                     nc.tensor.transpose(wt_ps[:, j, :], rows.bitcast(F32), ident[:])
                 nc.vector.tensor_copy(
@@ -332,7 +332,9 @@ def tile_share_lstm_cell_pa_kernel(
             for step in order:
                 step()
 
-        ctx.enter_context(tc.manual_schedule(engines={mybir.EngineType.PE}))
+        ctx.enter_context(
+            tc.manual_schedule(engines={mybir.EngineType.PE, mybir.EngineType.Activation, mybir.EngineType.DVE})
+        )
         for t in range(TILES_HALF):
             transpose_x(t)
         transpose_bias()

@@ -31,6 +31,9 @@ FLOPS = 2 * ROWS * GATES * (DI + DH)
 
 VECTOR_COPIES = ((1, 3, 5, 7, 9, 11, 13), (0, 1, 2, 4, 5, 6, 8, 9, 10, 12, 13))
 
+IDLE_FIRST = 4
+IDLE_LAST = 4
+
 
 def tile_share_lstm_cell_pa_kernel(
     tc,
@@ -74,6 +77,8 @@ def tile_share_lstm_cell_pa_kernel(
         nc.vector.memset(warm_in[:], 0.0)
         warm_out = keep.tile([P, 1], F32)
         nc.scalar.activation(out=warm_out[:], in_=warm_in[:], func=ACT.Sigmoid)
+        idle_sb = keep.tile([P, BANK], BF16)
+        nc.vector.memset(idle_sb[:], 0.0)
         w_scales = keep.tile([P, PASSES, GATES], U8, align_bytes=64)
         nc.vector.memset(w_scales[:].rearrange("p g n -> p (g n)").bitcast(I32), 0)
         bias_x_rows = keep.tile([P, P], BF16)
@@ -335,9 +340,18 @@ def tile_share_lstm_cell_pa_kernel(
         ctx.enter_context(
             tc.manual_schedule(engines={mybir.EngineType.PE, mybir.EngineType.Activation, mybir.EngineType.DVE})
         )
+        idle_ps = psum_sum.tile([P, BANK], F32, tag="bank")
+
+        def keep_busy(times):
+            for i in range(times):
+                nc.tensor.matmul(idle_ps[:], lhsT=idle_sb[:, 0:P], rhs=idle_sb[:], start=True, stop=True)
+
+        keep_busy(IDLE_FIRST)
         for t in range(TILES_HALF):
             transpose_x(t)
+            keep_busy(1)
         transpose_bias()
+        keep_busy(IDLE_LAST)
         for j in range(GATE_TILES):
             mx_product(0, j)
             if j == 6:

@@ -285,51 +285,56 @@ def tile_share_lstm_cell_pa_kernel(
 
             return [step_kept, step_new, step_c, step_b01, step_b2]
 
-        def share_steps(t):
-            res, cell, b_o = work[t]
-            o_g = gates[t][:, 2 * DH : 3 * DH]
+        def share_steps(t, cols, stores):
+            res, cell_all, b_o = work[t]
+            cell = cell_all[:, cols]
+            o_g = gates[t][:, 2 * DH + cols.start : 2 * DH + cols.stop]
             rest1 = temps.tile([P, DH], F32)
             part2 = temps.tile([P, DH], F32)
             rest2 = temps.tile([P, DH], F32)
 
             def store(k):
-                nc.sync.dma_start(out=out_views[k][:, t, :], in_=res[:, k, :])
+                if stores:
+                    nc.sync.dma_start(out=out_views[k][:, t, :], in_=res[:, k, :])
 
             def step_s0():
-                fused(res[:, 2, :], b_o[:, 0, :], 1.0, cell[:], ALU.add, ALU.mult)
+                fused(res[:, 2, cols], b_o[:, 0, cols], 1.0, cell, ALU.add, ALU.mult)
                 store(2)
 
             def step_rest1():
-                fused(rest1[:], b_o[:, 1, :], 2.0, res[:, 2, :], ALU.add, ALU.subtract)
+                fused(rest1[:, cols], b_o[:, 1, cols], 2.0, res[:, 2, cols], ALU.add, ALU.subtract)
 
             def step_s1():
-                fused(res[:, 3, :], rest1[:], 0.5, cell[:], ALU.mult, ALU.mult)
+                fused(res[:, 3, cols], rest1[:, cols], 0.5, cell, ALU.mult, ALU.mult)
                 store(3)
 
             def step_part2():
-                fused(part2[:], res[:, 2, :], -2.0, b_o[:, 2, :], ALU.mult, ALU.add)
+                fused(part2[:, cols], res[:, 2, cols], -2.0, b_o[:, 2, cols], ALU.mult, ALU.add)
 
             def step_rest2():
-                fused(rest2[:], part2[:], 3.0, res[:, 3, :], ALU.add, ALU.subtract)
+                fused(rest2[:, cols], part2[:, cols], 3.0, res[:, 3, cols], ALU.add, ALU.subtract)
 
             def step_s2():
-                fused(res[:, 4, :], rest2[:], 1.0 / 3.0, cell[:], ALU.mult, ALU.mult)
+                fused(res[:, 4, cols], rest2[:, cols], 1.0 / 3.0, cell, ALU.mult, ALU.mult)
                 store(4)
 
             def step_h():
-                nc.vector.tensor_tensor(out=res[:, 0, :], in0=o_g, in1=cell[:], op=ALU.mult)
+                nc.vector.tensor_tensor(out=res[:, 0, cols], in0=o_g, in1=cell, op=ALU.mult)
                 store(0)
 
             return [step_s0, step_rest1, step_s1, step_part2, step_rest2, step_s2, step_h]
 
         def finish(t):
             first = cell_steps(t) if t < TILES else []
-            second = share_steps(t - 1) if t > 0 else []
-            if not second:
+            second = share_steps(t - 1, slice(0, DH), True) if 0 < t < TILES else []
+            if t == 0:
                 order = first
-            elif not first:
-                s_0, r_1, s_1, p_2, r_2, s_2, h_t = second
-                order = [s_0, h_t, r_1, p_2, s_1, r_2, s_2]
+            elif t == TILES:
+                left = share_steps(t - 1, slice(0, DH // 2), False)
+                right = share_steps(t - 1, slice(DH // 2, DH), True)
+                order = []
+                for n in (0, 6, 1, 3, 2, 4, 5):
+                    order.extend([left[n], right[n]])
             else:
                 kept, new, c_t, b01, b_2 = first
                 s_0, r_1, s_1, p_2, r_2, s_2, h_t = second

@@ -176,6 +176,10 @@ def tile_share_lstm_cell_pa_kernel(
                     )
             grouped = stage.tile([P, PASSES, P, 4], BF16, align_bytes=64)
             nc.scalar.copy(out=grouped[:].bitcast(F32), in_=xt_ps[:].rearrange("p g u r -> p g r u"))
+            return grouped
+
+        def quantize_x(t, grouped):
+            half, place = divmod(t, TILES_HALF)
             for g in range(PASSES):
                 nc.vector.quantize_mx(
                     out=x_codes[:, half, g, place * P : (place + 1) * P].bitcast(FP8X4),
@@ -353,7 +357,7 @@ def tile_share_lstm_cell_pa_kernel(
 
         keep_busy(IDLE_FIRST)
         for t in range(TILES_HALF):
-            transpose_x(t)
+            quantize_x(t, transpose_x(t))
             keep_busy(1)
         transpose_bias()
         keep_busy(IDLE_LAST)
@@ -365,29 +369,33 @@ def tile_share_lstm_cell_pa_kernel(
                 transpose_states(0)
                 transpose_states(1)
         gate_sums(0)
-        finish(0)
-        transpose_x(4)
+        x_4 = transpose_x(4)
         transpose_states(2)
+        finish(0)
+        quantize_x(4, x_4)
         gate_sums(1)
-        finish(1)
-        transpose_x(5)
+        x_5 = transpose_x(5)
         transpose_states(3)
+        finish(1)
+        quantize_x(5, x_5)
         gate_sums(2)
+        x_6 = transpose_x(6)
+        x_7 = transpose_x(7)
         finish(2)
-        transpose_x(6)
-        transpose_x(7)
+        quantize_x(6, x_6)
+        quantize_x(7, x_7)
         gate_sums(3)
-        finish(3)
         transpose_states(4)
         transpose_states(5)
+        finish(3)
         for j in range(GATE_TILES):
             mx_product(1, j)
         gate_sums(4)
-        finish(4)
         transpose_states(6)
+        finish(4)
         gate_sums(5)
-        finish(5)
         transpose_states(7)
+        finish(5)
         gate_sums(6)
         finish(6)
         gate_sums(7)

@@ -18,21 +18,28 @@ ROWS = 1024
 DI = 1024
 DH = 256
 TILES = ROWS // P
-HALVES = 2
-TILES_HALF = TILES // HALVES
+MX_GROUPS = ((0,), (1, 2, 3, 4), (5,), (6,), (7,))
 LSTM = 4 * DH
 GATES = 7 * DH
 GATE_TILES = GATES // P
+HALF_BLOCKS = GATE_TILES // 2
 K_PASS = 4 * P
 PASSES = DI // K_PASS
 BANK = 512
 
+MX_STEPS = (
+    [(1, (j,)) for j in range(GATE_TILES)],
+    [],
+    [(2, (0, 1, 2, 3)), (2, (4, 5, 6))],
+    [(2, (7, 8, 9, 10)), (2, (11, 12, 13))],
+    [(3, (0, 1, 2, 3)), (3, (4, 5, 6)), (3, (7, 8, 9, 10)), (3, (11, 12, 13))],
+    [(4, (0, 1, 2, 3)), (4, (4, 5, 6))],
+    [(4, (7, 8, 9, 10)), (4, (11, 12, 13))],
+    [],
+)
+X_STEPS = {1: 5, 2: 6, 3: 7}
+
 FLOPS = 2 * ROWS * GATES * (DI + DH)
-
-VECTOR_COPIES = ((1, 3, 5, 7, 9, 11, 13), (0, 1, 2, 4, 5, 6, 8, 9, 10, 12, 13))
-
-IDLE_FIRST = 4
-IDLE_LAST = 4
 
 
 def tile_share_lstm_cell_pa_kernel(
@@ -65,82 +72,91 @@ def tile_share_lstm_cell_pa_kernel(
     with ExitStack() as ctx:
         keep = ctx.enter_context(tc.tile_pool(name="keep", bufs=1))
         stage = ctx.enter_context(tc.tile_pool(name="stage", bufs=3))
-        chain = ctx.enter_context(tc.tile_pool(name="chain", bufs=4))
+        chain = ctx.enter_context(tc.tile_pool(name="chain", bufs=3))
         temps = ctx.enter_context(tc.tile_pool(name="temps", bufs=2))
         results = ctx.enter_context(tc.tile_pool(name="results", bufs=3))
-        psum_tr = ctx.enter_context(tc.psum_pool(name="psum_tr", bufs=2))
-        psum_sum = ctx.enter_context(tc.psum_pool(name="psum_sum", bufs=6))
+        psum_tr = ctx.enter_context(tc.psum_pool(name="psum_tr", bufs=1))
+        psum_mx = ctx.enter_context(tc.psum_pool(name="psum_mx", bufs=3))
+        psum_sum = ctx.enter_context(tc.psum_pool(name="psum_sum", bufs=4))
 
-        ident = keep.tile([P, P], F32)
-        make_identity(nc, ident[:])
-        warm_in = keep.tile([P, 1], F32)
-        nc.vector.memset(warm_in[:], 0.0)
-        warm_out = keep.tile([P, 1], F32)
-        nc.scalar.activation(out=warm_out[:], in_=warm_in[:], func=ACT.Sigmoid)
-        idle_sb = keep.tile([P, BANK], BF16)
-        nc.vector.memset(idle_sb[:], 0.0)
         w_scales = keep.tile([P, PASSES, GATES], U8, align_bytes=64)
         nc.vector.memset(w_scales[:].rearrange("p g n -> p (g n)").bitcast(I32), 0)
         bias_x_rows = keep.tile([P, P], BF16)
         nc.vector.memset(bias_x_rows[:], 0.0)
         bias_s_rows = keep.tile([P, P], BF16)
         nc.vector.memset(bias_s_rows[:], 0.0)
-
-        nc.scalar.dma_start(out=bias_x_rows[0:GATE_TILES, :], in_=bias_ih.rearrange("(j p) -> j p", p=P))
-        nc.scalar.dma_start(out=bias_s_rows[0 : LSTM // P, :], in_=bias_hh.rearrange("(j p) -> j p", p=P))
-        for i, bias_sh in enumerate((bias_sh0, bias_sh1, bias_sh2)):
-            first = (LSTM + i * DH) // P
-            nc.scalar.dma_start(
-                out=bias_s_rows[first : first + DH // P, :], in_=bias_sh.rearrange("(j p) -> j p", p=P)
-            )
-        mask_bf = keep.tile([P, TILES], BF16)
-        nc.scalar.dma_start(out=mask_bf[:], in_=mask.rearrange("(p t) -> p t", t=TILES))
-        c_sb = keep.tile([P, TILES, DH], BF16)
-        nc.gpsimd.dma_start(out=c_sb[:], in_=c_minors.rearrange("(p t) d -> p t d", t=TILES))
+        idle_sb = keep.tile([P, BANK], BF16)
+        nc.vector.memset(idle_sb[:], 0.0)
+        warm_in = keep.tile([P, 1], F32)
+        nc.vector.memset(warm_in[:], 0.0)
+        warm_out = keep.tile([P, 1], F32)
+        nc.scalar.activation(out=warm_out[:], in_=warm_in[:], func=ACT.Sigmoid)
 
         x_sb = keep.tile([P, TILES, DI], BF16)
         x_view = x.rearrange("(p t) k -> p t k", t=TILES)
         state_views = [s.rearrange("(p t) d -> p t d", t=TILES) for s in (h_minors, s0, s1, s2)]
         state_sb = [keep.tile([P, TILES, DH], BF16, name="state_sb%d" % j) for j in range(4)]
 
-        def load_x(half):
-            for t in range(half * TILES_HALF, (half + 1) * TILES_HALF):
-                nc.sync.dma_start(out=x_sb[:, t, :], in_=x_view[:, t, :])
+        def load_x(first, last):
+            nc.sync.dma_start(out=x_sb[:, first:last, :], in_=x_view[:, first:last, :])
 
-        def load_states(half):
-            four = slice(half * TILES_HALF, (half + 1) * TILES_HALF)
+        def load_states(first, last):
             for j in range(4):
-                nc.sync.dma_start(out=state_sb[j][:, four, :], in_=state_views[j][:, four, :])
+                nc.sync.dma_start(out=state_sb[j][:, first:last, :], in_=state_views[j][:, first:last, :])
 
-        load_x(0)
-        w_words = keep.tile([P, PASSES, 2 * GATES], U8, align_bytes=64)
+        load_x(0, 1)
         for quad in range(4):
             nc.sync.dma_start(
                 out=w_scales[32 * quad : 32 * quad + 4, :, :].bitcast(I32),
                 in_=weight_ih_scales[:, 4 * quad : 4 * quad + 4, :].bitcast(I32).rearrange("g r n -> r g n"),
             )
+        w_words = keep.tile([P, 2, PASSES, GATES], U8, align_bytes=64)
         for part in range(2):
             some = slice(part * GATES, (part + 1) * GATES)
-            for g in range(PASSES):
-                nc.sync.dma_start(out=w_words[:, g, some].bitcast(I32), in_=weight_ih_words[g][:, some].bitcast(I32))
+            nc.sync.dma_start(
+                out=w_words[:, part, :, :].bitcast(I32),
+                in_=weight_ih_words[:, :, some].bitcast(I32).rearrange("g p n -> p g n"),
+            )
+        nc.sync.dma_start(out=bias_x_rows[0:GATE_TILES, :], in_=bias_ih.rearrange("(j p) -> j p", p=P))
+        nc.sync.dma_start(out=bias_s_rows[0 : LSTM // P, :], in_=bias_hh.rearrange("(j p) -> j p", p=P))
+        for i, bias_sh in enumerate((bias_sh0, bias_sh1, bias_sh2)):
+            first = (LSTM + i * DH) // P
+            nc.sync.dma_start(out=bias_s_rows[first : first + DH // P, :], in_=bias_sh.rearrange("(j p) -> j p", p=P))
+        load_states(0, 2)
+        load_x(1, 3)
+        load_x(3, 5)
+        load_states(2, 4)
+        load_x(5, TILES)
+        load_states(4, TILES)
+
         whh_sb = keep.tile([P, LSTM // P, DH], BF16)
-        nc.sync.dma_start(out=whh_sb[:], in_=weight_hh.rearrange("(j p) k -> p j k", p=P))
+        nc.gpsimd.dma_start(out=whh_sb[:], in_=weight_hh.rearrange("(j p) k -> p j k", p=P))
+        ident = keep.tile([P, P], F32)
+        make_identity(nc, ident[:])
         weight_row_tiles = [whh_sb[:, j, :] for j in range(LSTM // P)]
         for i, weight_sh in enumerate((weight_sh0, weight_sh1, weight_sh2)):
             wsh_sb = keep.tile([P, DH // P, DH], BF16, name="wsh_sb%d" % i)
-            nc.sync.dma_start(out=wsh_sb[:], in_=weight_sh.rearrange("(j p) k -> p j k", p=P))
+            nc.gpsimd.dma_start(out=wsh_sb[:], in_=weight_sh.rearrange("(j p) k -> p j k", p=P))
             weight_row_tiles.extend([wsh_sb[:, j, :] for j in range(DH // P)])
-        load_states(0)
-        load_x(1)
-        load_states(1)
+        mask_bf = keep.tile([P, TILES], BF16)
+        nc.gpsimd.dma_start(out=mask_bf[:], in_=mask.rearrange("(p t) -> p t", t=TILES))
+        c_sb = keep.tile([P, TILES, DH], BF16)
+        nc.gpsimd.dma_start(out=c_sb[:], in_=c_minors.rearrange("(p t) d -> p t d", t=TILES))
 
-        mask_f = keep.tile([P, TILES], F32)
-        nc.vector.tensor_copy(out=mask_f[:], in_=mask_bf[:])
+        factors = keep.tile([P, 3, TILES], F32)
+
+        def prepare_factors():
+            nc.vector.tensor_copy(out=factors[:, 0, :], in_=mask_bf[:])
+            for n in range(1, 3):
+                nc.vector.tensor_scalar(
+                    out=factors[:, n, :], in0=mask_bf[:], scalar1=1.0 / (n + 1), scalar2=None, op0=ALU.mult
+                )
+
         bias_rows = keep.tile([P, P], F32)
-        nc.vector.tensor_tensor(out=bias_rows[:], in0=bias_x_rows[:], in1=bias_s_rows[:], op=ALU.add)
         bias_col = keep.tile([P, GATE_TILES], F32)
 
         def transpose_bias():
+            nc.vector.tensor_tensor(out=bias_rows[:], in0=bias_x_rows[:], in1=bias_s_rows[:], op=ALU.add)
             bias_ps = psum_tr.tile([P, 4, P], F32, tag="tr")
             nc.tensor.transpose(bias_ps[:, 0, :], bias_rows[:], ident[:])
             nc.vector.tensor_copy(out=bias_col[:], in_=bias_ps[:, 0, 0:GATE_TILES])
@@ -148,77 +164,92 @@ def tile_share_lstm_cell_pa_kernel(
         w_t = keep.tile([P, GATES], F32)
         w_t_halves = w_t[:].bitcast(BF16).rearrange("p (n e) -> p n e", e=2)
 
-        def transpose_weights():
-            for first in range(0, len(weight_row_tiles), 4):
-                group = weight_row_tiles[first : first + 4]
-                wt_ps = psum_sum.tile([P, 4, P], F32, tag="bank")
-                for j, rows in enumerate(group):
-                    nc.tensor.transpose(wt_ps[:, j, :], rows.bitcast(F32), ident[:])
-                nc.vector.tensor_copy(
-                    out=w_t[:, first * P : (first + len(group)) * P],
-                    in_=wt_ps[:, 0 : len(group), :].rearrange("p j n -> p (j n)"),
-                )
+        def transpose_weights(first, last, copy):
+            group = weight_row_tiles[first:last]
+            wt_ps = psum_sum.tile([P, 4, P], F32, tag="sum")
+            for j, rows in enumerate(group):
+                nc.tensor.transpose(wt_ps[:, j, :], rows.bitcast(F32), ident[:])
+            copy(
+                out=w_t[:, first * P : last * P],
+                in_=wt_ps[:, 0 : len(group), :].rearrange("p j n -> p (j n)"),
+            )
 
-        x_codes = keep.tile([P, HALVES, PASSES, TILES_HALF * P], U32, align_bytes=64)
-        x_scales = keep.tile([P, HALVES, PASSES, TILES_HALF * P], U8, align_bytes=64)
+        x_codes = [keep.tile([P, PASSES, len(m) * P], U32, align_bytes=64, name="x_codes%d" % n) for n, m in enumerate(MX_GROUPS)]
+        x_scales = [keep.tile([P, PASSES, len(m) * P], U8, align_bytes=64, name="x_scales%d" % n) for n, m in enumerate(MX_GROUPS)]
+        home = {t: (n, m.index(t)) for n, m in enumerate(MX_GROUPS) for t in m}
         states_t_sb = keep.tile([P, TILES, 4, P], F32)
-        mx_sb = keep.tile([P, HALVES, GATE_TILES, BANK], F32)
+        mx_sb = [keep.tile([P, GATE_TILES, len(m) * P], F32, name="mx_sb%d" % n) for n, m in enumerate(MX_GROUPS)]
         gates = {}
+        grouped_x = {}
 
-        def transpose_x(t):
-            half, place = divmod(t, TILES_HALF)
+        def transpose_x(t, copy, pool, tag):
             x_words = x_sb[:, t, :].bitcast(F32)
-            xt_ps = psum_tr.tile([P, PASSES, 2, P], F32, tag="tr")
+            xt_ps = pool.tile([P, PASSES, 2, P], F32, tag=tag)
             for g in range(PASSES):
                 for u in range(2):
                     nc.tensor.transpose(
                         xt_ps[:, g, u, :], x_words[:, (K_PASS // 2) * g + u : (K_PASS // 2) * (g + 1) : 2], ident[:]
                     )
             grouped = stage.tile([P, PASSES, P, 4], BF16, align_bytes=64)
-            nc.scalar.copy(out=grouped[:].bitcast(F32), in_=xt_ps[:].rearrange("p g u r -> p g r u"))
-            return grouped
+            copy(out=grouped[:].bitcast(F32), in_=xt_ps[:].rearrange("p g u r -> p g r u"))
+            grouped_x[t] = grouped
 
-        def quantize_x(t, grouped):
-            half, place = divmod(t, TILES_HALF)
+        def quantize_x(t):
+            group, place = home[t]
             for g in range(PASSES):
                 nc.vector.quantize_mx(
-                    out=x_codes[:, half, g, place * P : (place + 1) * P].bitcast(FP8X4),
-                    scales=x_scales[:, half, g, place * P : (place + 1) * P],
-                    in_=grouped[:, g, :, :].rearrange("p r k -> p (r k)"),
+                    out=x_codes[group][:, g, place * P : (place + 1) * P].bitcast(FP8X4),
+                    scales=x_scales[group][:, g, place * P : (place + 1) * P],
+                    in_=grouped_x[t][:, g, :, :].rearrange("p r k -> p (r k)"),
                 )
 
-        def transpose_states(t):
-            st_ps = psum_tr.tile([P, 4, P], F32, tag="tr")
+        def transpose_states(t, pool, tag):
+            st_ps = pool.tile([P, 4, P], F32, tag=tag)
             for j in range(4):
                 nc.tensor.transpose(st_ps[:, j, :], state_sb[j][:, t, :].bitcast(F32), ident[:])
             nc.scalar.copy(out=states_t_sb[:, t, :, :], in_=st_ps[:])
 
-        def mx_product(half, j):
-            acc = psum_sum.tile([P, BANK], F32, tag="bank")
-            for g in range(PASSES):
-                nc.tensor.matmul_mx(
-                    out=acc[:],
-                    lhsT=w_words[:, g, 2 * P * j : 2 * P * (j + 1)].bitcast(FP4X4),
-                    lhsT_scale=w_scales[:, g, P * j : P * (j + 1)],
-                    rhs=x_codes[:, half, g, :].bitcast(FP8X4),
-                    rhs_scale=x_scales[:, half, g, :],
-                    start=(g == 0),
-                    stop=(g == PASSES - 1),
-                )
-            if j in VECTOR_COPIES[half]:
-                nc.vector.tensor_scalar(
-                    out=mx_sb[:, half, j, :], in0=acc[:], scalar1=bias_col[:, j : j + 1], scalar2=None, op0=ALU.add
+        def mx_product(group, blocks, pool, tag):
+            rows = len(MX_GROUPS[group]) * P
+            acc = pool.tile([P, BANK // rows, rows], F32, tag=tag)
+            for n, j in enumerate(blocks):
+                for g in range(PASSES):
+                    nc.tensor.matmul_mx(
+                        out=acc[:, n, :],
+                        lhsT=w_words[:, j // HALF_BLOCKS, g, 2 * P * (j % HALF_BLOCKS) : 2 * P * (j % HALF_BLOCKS + 1)].bitcast(FP4X4),
+                        lhsT_scale=w_scales[:, g, P * j : P * (j + 1)],
+                        rhs=x_codes[group][:, g, :].bitcast(FP8X4),
+                        rhs_scale=x_scales[group][:, g, :],
+                        start=(g == 0),
+                        stop=(g == PASSES - 1),
+                    )
+            return acc
+
+        def mx_copy(group, blocks, acc, on_vector):
+            first, count = blocks[0], len(blocks)
+            rows = len(MX_GROUPS[group]) * P
+            if on_vector:
+                nc.vector.tensor_tensor(
+                    out=mx_sb[group][:, first : first + count, :],
+                    in0=acc[:, 0:count, :],
+                    in1=bias_col[:, first : first + count].unsqueeze(2).to_broadcast([P, count, rows]),
+                    op=ALU.add,
                 )
             else:
-                nc.scalar.activation(out=mx_sb[:, half, j, :], in_=acc[:], func=ACT.Identity, bias=bias_col[:, j : j + 1])
+                for n, j in enumerate(blocks):
+                    nc.scalar.activation(
+                        out=mx_sb[group][:, j, :], in_=acc[:, n, :], func=ACT.Identity, bias=bias_col[:, j : j + 1]
+                    )
 
-        def gate_sums(t):
-            half, place = divmod(t, TILES_HALF)
+        sums = {}
+
+        def plain_product(t):
             states_t = states_t_sb[:, t, :, :].bitcast(BF16).rearrange("p j (r e) -> p j r e", e=2)
-            gate = chain.tile([P, GATES], F32)
+            sums[t] = []
             for c0 in range(0, GATES, BANK):
                 width = min(BANK, GATES - c0)
-                total = psum_sum.tile([P, BANK], F32, tag="bank")
+                total = psum_sum.tile([P, BANK], F32, tag="sum")
+                sums[t].append(total)
                 step = BANK if c0 < LSTM else DH
                 for b0 in range(c0, c0 + width, step):
                     source = max(0, b0 // DH - 3)
@@ -227,25 +258,35 @@ def tile_share_lstm_cell_pa_kernel(
                             total[:, b0 - c0 : b0 - c0 + step],
                             lhsT=states_t[:, source, :, e],
                             rhs=w_t_halves[:, b0 : b0 + step, e],
-                            start=(e == 0),
+                            start=(b0 == c0 and e == 0),
                             stop=False,
                         )
-                    blocks = range(b0 // P, (b0 + step) // P)
-                    for j in blocks:
-                        nc.tensor.matmul(
-                            total[:, j * P - c0 : (j + 1) * P - c0],
-                            lhsT=mx_sb[:, half, j, place * P : (place + 1) * P],
-                            rhs=ident[:],
-                            is_transpose=True,
-                            start=False,
-                            stop=(j == blocks[-1]),
-                        )
+
+        def add_mx(t):
+            group, place = home[t]
+            for bank, c0 in enumerate(range(0, GATES, BANK)):
+                blocks = range(c0 // P, min(c0 + BANK, GATES) // P)
+                for j in blocks:
+                    nc.tensor.matmul(
+                        sums[t][bank][:, j * P - c0 : (j + 1) * P - c0],
+                        lhsT=mx_sb[group][:, j, place * P : (place + 1) * P],
+                        rhs=ident[:],
+                        is_transpose=True,
+                        start=False,
+                        stop=(j == blocks[-1]),
+                    )
+
+        def activate(t):
+            gate = chain.tile([P, GATES], F32)
+            gates[t] = gate
+            for bank, c0 in enumerate(range(0, GATES, BANK)):
+                width = min(BANK, GATES - c0)
+                total = sums[t][bank]
                 if c0 == 2 * DH:
                     nc.scalar.activation(out=gate[:, c0 : c0 + DH], in_=total[:, 0:DH], func=ACT.Sigmoid)
                     nc.scalar.activation(out=gate[:, c0 + DH : c0 + BANK], in_=total[:, DH:BANK], func=ACT.Tanh)
                 else:
                     nc.scalar.activation(out=gate[:, c0 : c0 + width], in_=total[:, 0:width], func=ACT.Sigmoid)
-            gates[t] = gate
 
         out_views = [o.rearrange("(p t) d -> p t d", t=TILES) for o in (out_0, out_1, out_2, out_3, out_4)]
 
@@ -256,14 +297,13 @@ def tile_share_lstm_cell_pa_kernel(
 
         def cell_steps(t):
             gate = gates[t]
-            m = mask_f[:, t : t + 1]
+            m = factors[:, 0, t : t + 1]
             res = results.tile([P, 5, DH], F32)
             kept = temps.tile([P, DH], F32)
             new = temps.tile([P, DH], F32)
             tanh_c = temps.tile([P, DH], F32)
-            cell = temps.tile([P, DH], F32)
             b_o = temps.tile([P, 3, DH], F32)
-            work[t] = (res, cell, b_o)
+            work[t] = (res, tanh_c, b_o)
             o_g = gate[:, 2 * DH : 3 * DH]
             b_g = gate[:, LSTM:GATES].rearrange("p (j d) -> p j d", j=3)
 
@@ -275,23 +315,20 @@ def tile_share_lstm_cell_pa_kernel(
 
             def step_c():
                 nc.vector.tensor_tensor(out=res[:, 1, :], in0=kept[:], in1=new[:], op=ALU.add)
+
+            def step_tanh():
                 nc.scalar.activation(out=tanh_c[:], in_=res[:, 1, :], func=ACT.Tanh)
-                nc.scalar.activation(out=cell[:], in_=tanh_c[:], func=ACT.Copy, scale=m)
                 nc.sync.dma_start(out=out_views[1][:, t, :], in_=res[:, 1, :])
 
-            def step_b01():
-                nc.vector.tensor_tensor(
-                    out=b_o[:, 0:2, :], in0=b_g[:, 0:2, :], in1=o_g.unsqueeze(1).to_broadcast([P, 2, DH]), op=ALU.subtract
-                )
+            def step_b():
+                fused(b_o[:], b_g, 1.0, o_g.unsqueeze(1).to_broadcast([P, 3, DH]), ALU.add, ALU.subtract)
 
-            def step_b2():
-                nc.vector.tensor_tensor(out=b_o[:, 2, :], in0=b_g[:, 2, :], in1=o_g, op=ALU.subtract)
-
-            return [step_kept, step_new, step_c, step_b01, step_b2]
+            return step_kept, step_new, step_c, step_tanh, step_b
 
         def share_steps(t, cols, stores):
-            res, cell_all, b_o = work[t]
-            cell = cell_all[:, cols]
+            res, tanh_c_all, b_o = work[t]
+            tanh_c = tanh_c_all[:, cols]
+            m1, m2, m3 = [factors[:, n, t : t + 1] for n in range(3)]
             o_g = gates[t][:, 2 * DH + cols.start : 2 * DH + cols.stop]
             rest1 = temps.tile([P, DH], F32)
             part2 = temps.tile([P, DH], F32)
@@ -302,102 +339,103 @@ def tile_share_lstm_cell_pa_kernel(
                     nc.sync.dma_start(out=out_views[k][:, t, :], in_=res[:, k, :])
 
             def step_s0():
-                fused(res[:, 2, cols], b_o[:, 0, cols], 1.0, cell, ALU.add, ALU.mult)
+                fused(res[:, 2, cols], b_o[:, 0, cols], m1, tanh_c, ALU.mult, ALU.mult)
                 store(2)
 
             def step_rest1():
-                fused(rest1[:, cols], b_o[:, 1, cols], 2.0, res[:, 2, cols], ALU.add, ALU.subtract)
+                fused(rest1[:, cols], b_o[:, 1, cols], 1.0, res[:, 2, cols], ALU.add, ALU.subtract)
 
             def step_s1():
-                fused(res[:, 3, cols], rest1[:, cols], 0.5, cell, ALU.mult, ALU.mult)
+                fused(res[:, 3, cols], rest1[:, cols], m2, tanh_c, ALU.mult, ALU.mult)
                 store(3)
 
             def step_part2():
                 fused(part2[:, cols], res[:, 2, cols], -2.0, b_o[:, 2, cols], ALU.mult, ALU.add)
 
             def step_rest2():
-                fused(rest2[:, cols], part2[:, cols], 3.0, res[:, 3, cols], ALU.add, ALU.subtract)
+                fused(rest2[:, cols], part2[:, cols], 2.0, res[:, 3, cols], ALU.add, ALU.subtract)
 
             def step_s2():
-                fused(res[:, 4, cols], rest2[:, cols], 1.0 / 3.0, cell, ALU.mult, ALU.mult)
+                fused(res[:, 4, cols], rest2[:, cols], m3, tanh_c, ALU.mult, ALU.mult)
                 store(4)
 
             def step_h():
-                nc.vector.tensor_tensor(out=res[:, 0, cols], in0=o_g, in1=cell, op=ALU.mult)
+                fused(res[:, 0, cols], o_g, m1, tanh_c, ALU.mult, ALU.mult)
                 store(0)
 
-            return [step_s0, step_rest1, step_s1, step_part2, step_rest2, step_s2, step_h]
-
-        def finish(t):
-            first = cell_steps(t) if t < TILES else []
-            second = share_steps(t - 1, slice(0, DH), True) if 0 < t < TILES else []
-            if t == 0:
-                order = first
-            elif t == TILES:
-                left = share_steps(t - 1, slice(0, DH // 2), False)
-                right = share_steps(t - 1, slice(DH // 2, DH), True)
-                order = []
-                for n in (0, 6, 1, 3, 2, 4, 5):
-                    order.extend([left[n], right[n]])
-            else:
-                kept, new, c_t, b01, b_2 = first
-                s_0, r_1, s_1, p_2, r_2, s_2, h_t = second
-                order = [s_0, kept, r_1, new, s_1, p_2, c_t, r_2, b01, s_2, h_t, b_2]
-            for step in order:
-                step()
+            return step_s0, step_h, step_rest1, step_s1, step_part2, step_rest2, step_s2
 
         ctx.enter_context(
             tc.manual_schedule(engines={mybir.EngineType.PE, mybir.EngineType.Activation, mybir.EngineType.DVE})
         )
-        idle_ps = psum_sum.tile([P, BANK], F32, tag="bank")
+        idle_ps = psum_mx.tile([P, BANK], F32, tag="mx")
 
         def keep_busy(times):
             for i in range(times):
                 nc.tensor.matmul(idle_ps[:], lhsT=idle_sb[:, 0:P], rhs=idle_sb[:], start=True, stop=True)
 
-        keep_busy(IDLE_FIRST)
-        for t in range(TILES_HALF):
-            quantize_x(t, transpose_x(t))
-            keep_busy(1)
+        SUM, MX, TR = (psum_sum, "sum"), (psum_mx, "mx"), (psum_tr, "tr")
+        SUM, MX, TR = (psum_sum, "sum"), (psum_mx, "mx"), (psum_tr, "tr")
+        keep_busy(4)
+        transpose_x(0, nc.scalar.copy, *SUM)
+        quantize_x(0)
+        keep_busy(2)
+        transpose_weights(0, 4, nc.scalar.copy)
+        transpose_weights(4, 8, nc.scalar.copy)
         transpose_bias()
-        keep_busy(IDLE_LAST)
-        for j in range(GATE_TILES):
-            mx_product(0, j)
-            if j == 6:
-                transpose_weights()
-            if j == 10:
-                transpose_states(0)
-                transpose_states(1)
-        gate_sums(0)
-        x_4 = transpose_x(4)
-        transpose_states(2)
-        finish(0)
-        quantize_x(4, x_4)
-        gate_sums(1)
-        x_5 = transpose_x(5)
-        transpose_states(3)
-        finish(1)
-        quantize_x(5, x_5)
-        gate_sums(2)
-        x_6 = transpose_x(6)
-        x_7 = transpose_x(7)
-        finish(2)
-        quantize_x(6, x_6)
-        quantize_x(7, x_7)
-        gate_sums(3)
-        transpose_states(4)
-        transpose_states(5)
-        finish(3)
-        for j in range(GATE_TILES):
-            mx_product(1, j)
-        gate_sums(4)
-        transpose_states(6)
-        finish(4)
-        gate_sums(5)
-        transpose_states(7)
-        finish(5)
-        gate_sums(6)
-        finish(6)
-        gate_sums(7)
-        finish(7)
-        finish(8)
+        keep_busy(2)
+        for n, blocks in enumerate(((0, 1, 2, 3), (4, 5, 6), (7, 8, 9, 10), (11, 12, 13))):
+            acc = mx_product(0, blocks, *MX)
+            mx_copy(0, blocks, acc, n % 2 == 0)
+        transpose_states(0, *SUM)
+        transpose_states(1, *TR)
+        transpose_weights(8, 12, nc.vector.tensor_copy)
+        transpose_weights(12, 14, nc.vector.tensor_copy)
+        transpose_x(1, nc.scalar.copy, *MX)
+        transpose_x(2, nc.vector.tensor_copy, *MX)
+        quantize_x(1)
+        quantize_x(2)
+        plain_product(0)
+        transpose_x(3, nc.scalar.copy, *MX)
+        transpose_x(4, nc.vector.tensor_copy, *TR)
+        quantize_x(3)
+        quantize_x(4)
+        prepare_factors()
+        for t in range(TILES):
+            add_mx(t)
+            activate(t)
+            kept, new, c_t, tanh, b_o = cell_steps(t)
+            if t in X_STEPS:
+                transpose_x(X_STEPS[t], nc.scalar.copy, *TR)
+            if t:
+                s_0, h_t, r_1, s_1, p_2, r_2, s_2 = share_steps(t - 1, slice(0, DH), True)
+                early = (s_0, h_t, r_1)
+                for step in early:
+                    step()
+            kept()
+            for n, (group, blocks) in enumerate(MX_STEPS[t]):
+                acc = mx_product(group, blocks, *MX)
+                mx_copy(group, blocks, acc, n < 4 or n % 2 == 0 if t == 0 else n < 1 and t < 4)
+                if n == (5 if t == 0 else 0):
+                    new()
+            if not MX_STEPS[t]:
+                new()
+            c_t()
+            tanh()
+            if t:
+                s_1()
+            b_o()
+            if t:
+                for step in (p_2, r_2, s_2):
+                    step()
+            if t in X_STEPS:
+                quantize_x(X_STEPS[t])
+            if t + 2 < TILES:
+                transpose_states(t + 2, *MX)
+            if t + 1 < TILES:
+                plain_product(t + 1)
+        left = share_steps(TILES - 1, slice(0, DH // 2), False)
+        right = share_steps(TILES - 1, slice(DH // 2, DH), True)
+        for a, b in zip(left, right):
+            a()
+            b()

@@ -18,7 +18,9 @@ ROWS = 1024
 DI = 1024
 DH = 256
 TILES = ROWS // P
-MX_GROUPS = ((0,), (1, 2, 3, 4), (5,), (6,), (7,))
+HALVES = 2
+TILES_HALF = TILES // HALVES
+HALF = ROWS // HALVES
 LSTM = 4 * DH
 GATES = 7 * DH
 GATE_TILES = GATES // P
@@ -27,17 +29,8 @@ K_PASS = 4 * P
 PASSES = DI // K_PASS
 BANK = 512
 
-MX_STEPS = (
-    [(1, (j,)) for j in range(GATE_TILES)],
-    [],
-    [(2, (0, 1, 2, 3)), (2, (4, 5, 6))],
-    [(2, (7, 8, 9, 10)), (2, (11, 12, 13))],
-    [(3, (0, 1, 2, 3)), (3, (4, 5, 6)), (3, (7, 8, 9, 10)), (3, (11, 12, 13))],
-    [(4, (0, 1, 2, 3)), (4, (4, 5, 6))],
-    [(4, (7, 8, 9, 10)), (4, (11, 12, 13))],
-    [],
-)
-X_STEPS = {1: 5, 2: 6, 3: 7}
+MX_CHUNKS = ((0, 1, 2, 3), (4, 5, 6, 7), (8, 9, 10), (11, 12, 13), (), (), (), ())
+QUAD = 32
 
 FLOPS = 2 * ROWS * GATES * (DI + DH)
 
@@ -92,10 +85,13 @@ def tile_share_lstm_cell_pa_kernel(
         warm_out = keep.tile([P, 1], F32)
         nc.scalar.activation(out=warm_out[:], in_=warm_in[:], func=ACT.Sigmoid)
 
-        x_sb = keep.tile([P, TILES, DI], BF16)
-        x_view = x.rearrange("(p t) k -> p t k", t=TILES)
-        state_views = [s.rearrange("(p t) d -> p t d", t=TILES) for s in (h_minors, s0, s1, s2)]
-        state_sb = [keep.tile([P, TILES, DH], BF16, name="state_sb%d" % j) for j in range(4)]
+        x_sb = keep.tile([P, TILES_HALF, DI], BF16)
+        x_view = x.rearrange("(t p) k -> p t k", p=P)
+        states = (h_minors, s0, s1, s2)
+        state_views = [s.rearrange("(t p) d -> p t d", p=P) for s in states]
+        state_sb = [keep.tile([P, TILES_HALF, DH], BF16, name="state_sb%d" % j) for j in range(4)]
+        x_quads = keep.tile([P, PASSES, HALF // QUAD, P], BF16, align_bytes=64)
+        state_quads = [keep.tile([P, HALF // QUAD, DH // 4], BF16, align_bytes=64, name="state_quads%d" % j) for j in range(4)]
 
         def load_x(first, last):
             nc.sync.dma_start(out=x_sb[:, first:last, :], in_=x_view[:, first:last, :])
@@ -104,62 +100,82 @@ def tile_share_lstm_cell_pa_kernel(
             for j in range(4):
                 nc.sync.dma_start(out=state_sb[j][:, first:last, :], in_=state_views[j][:, first:last, :])
 
+        def load_x_quads():
+            view = x[HALF:ROWS, :].rearrange("(b j) (g r w) -> g r j b w", j=QUAD, g=PASSES, r=4)
+            for g in range(PASSES):
+                for r in range(4):
+                    nc.sync.dma_start(out=x_quads[QUAD * r : QUAD * (r + 1), g, :, :], in_=view[g, r])
+
+        def load_state_quads():
+            for n in range(4):
+                view = states[n][HALF:ROWS, :].rearrange("(b j) (r w) -> r j b w", j=QUAD, r=4)
+                for r in range(4):
+                    nc.sync.dma_start(out=state_quads[n][QUAD * r : QUAD * (r + 1), :, :], in_=view[r])
+
         load_x(0, 1)
+        load_x(1, 2)
         for quad in range(4):
             nc.sync.dma_start(
                 out=w_scales[32 * quad : 32 * quad + 4, :, :].bitcast(I32),
                 in_=weight_ih_scales[:, 4 * quad : 4 * quad + 4, :].bitcast(I32).rearrange("g r n -> r g n"),
             )
+        load_x(2, 4)
         w_words = keep.tile([P, 2, PASSES, GATES], U8, align_bytes=64)
-        for part in range(2):
+
+        def load_words(part):
             some = slice(part * GATES, (part + 1) * GATES)
             nc.sync.dma_start(
                 out=w_words[:, part, :, :].bitcast(I32),
                 in_=weight_ih_words[:, :, some].bitcast(I32).rearrange("g p n -> p g n"),
             )
+
+        load_words(0)
         nc.sync.dma_start(out=bias_x_rows[0:GATE_TILES, :], in_=bias_ih.rearrange("(j p) -> j p", p=P))
+        nc.sync.dma_start(
+            out=bias_x_rows[GATE_TILES : GATE_TILES + TILES, :], in_=mask.rearrange("(t p) -> t p", p=P)
+        )
         nc.sync.dma_start(out=bias_s_rows[0 : LSTM // P, :], in_=bias_hh.rearrange("(j p) -> j p", p=P))
         for i, bias_sh in enumerate((bias_sh0, bias_sh1, bias_sh2)):
             first = (LSTM + i * DH) // P
             nc.sync.dma_start(out=bias_s_rows[first : first + DH // P, :], in_=bias_sh.rearrange("(j p) -> j p", p=P))
+        load_words(1)
         load_states(0, 2)
-        load_x(1, 3)
-        load_x(3, 5)
+        load_x_quads()
         load_states(2, 4)
-        load_x(5, TILES)
-        load_states(4, TILES)
+        load_state_quads()
 
-        whh_sb = keep.tile([P, LSTM // P, DH], BF16)
-        nc.gpsimd.dma_start(out=whh_sb[:], in_=weight_hh.rearrange("(j p) k -> p j k", p=P))
         ident = keep.tile([P, P], F32)
         make_identity(nc, ident[:])
+        whh_sb = keep.tile([P, LSTM // P, DH], BF16)
+        nc.gpsimd.dma_start(out=whh_sb[:], in_=weight_hh.rearrange("(j p) k -> p j k", p=P))
         weight_row_tiles = [whh_sb[:, j, :] for j in range(LSTM // P)]
         for i, weight_sh in enumerate((weight_sh0, weight_sh1, weight_sh2)):
             wsh_sb = keep.tile([P, DH // P, DH], BF16, name="wsh_sb%d" % i)
             nc.gpsimd.dma_start(out=wsh_sb[:], in_=weight_sh.rearrange("(j p) k -> p j k", p=P))
             weight_row_tiles.extend([wsh_sb[:, j, :] for j in range(DH // P)])
-        mask_bf = keep.tile([P, TILES], BF16)
-        nc.gpsimd.dma_start(out=mask_bf[:], in_=mask.rearrange("(p t) -> p t", t=TILES))
         c_sb = keep.tile([P, TILES, DH], BF16)
-        nc.gpsimd.dma_start(out=c_sb[:], in_=c_minors.rearrange("(p t) d -> p t d", t=TILES))
-
-        factors = keep.tile([P, 3, TILES], F32)
-
-        def prepare_factors():
-            nc.vector.tensor_copy(out=factors[:, 0, :], in_=mask_bf[:])
-            for n in range(1, 3):
-                nc.vector.tensor_scalar(
-                    out=factors[:, n, :], in0=mask_bf[:], scalar1=1.0 / (n + 1), scalar2=None, op0=ALU.mult
-                )
+        nc.gpsimd.dma_start(out=c_sb[:], in_=c_minors.rearrange("(t p) d -> p t d", p=P))
 
         bias_rows = keep.tile([P, P], F32)
-        bias_col = keep.tile([P, GATE_TILES], F32)
+        columns = keep.tile([P, GATE_TILES + TILES], F32)
+        bias_col = columns[:, 0:GATE_TILES]
+        factors = keep.tile([P, 3, TILES], F32)
 
         def transpose_bias():
             nc.vector.tensor_tensor(out=bias_rows[:], in0=bias_x_rows[:], in1=bias_s_rows[:], op=ALU.add)
             bias_ps = psum_tr.tile([P, 4, P], F32, tag="tr")
             nc.tensor.transpose(bias_ps[:, 0, :], bias_rows[:], ident[:])
-            nc.vector.tensor_copy(out=bias_col[:], in_=bias_ps[:, 0, 0:GATE_TILES])
+            nc.vector.tensor_copy(out=columns[:], in_=bias_ps[:, 0, 0 : GATE_TILES + TILES])
+
+        def prepare_factors():
+            for n in range(3):
+                nc.vector.tensor_scalar(
+                    out=factors[:, n, :],
+                    in0=columns[:, GATE_TILES : GATE_TILES + TILES],
+                    scalar1=1.0 / (n + 1),
+                    scalar2=None,
+                    op0=ALU.mult,
+                )
 
         w_t = keep.tile([P, GATES], F32)
         w_t_halves = w_t[:].bitcast(BF16).rearrange("p (n e) -> p n e", e=2)
@@ -174,11 +190,11 @@ def tile_share_lstm_cell_pa_kernel(
                 in_=wt_ps[:, 0 : len(group), :].rearrange("p j n -> p (j n)"),
             )
 
-        x_codes = [keep.tile([P, PASSES, len(m) * P], U32, align_bytes=64, name="x_codes%d" % n) for n, m in enumerate(MX_GROUPS)]
-        x_scales = [keep.tile([P, PASSES, len(m) * P], U8, align_bytes=64, name="x_scales%d" % n) for n, m in enumerate(MX_GROUPS)]
-        home = {t: (n, m.index(t)) for n, m in enumerate(MX_GROUPS) for t in m}
-        states_t_sb = keep.tile([P, TILES, 4, P], F32)
-        mx_sb = [keep.tile([P, GATE_TILES, len(m) * P], F32, name="mx_sb%d" % n) for n, m in enumerate(MX_GROUPS)]
+        x_codes = keep.tile([P, HALVES, PASSES, HALF], U32, align_bytes=64)
+        x_scales = keep.tile([P, HALVES, PASSES, HALF], U8, align_bytes=64)
+        states_t_first = keep.tile([P, TILES_HALF, 4, P], F32)
+        states_t_second = keep.tile([P, 4, HALF], F32, align_bytes=64)
+        mx_sb = keep.tile([P, HALVES, GATE_TILES, HALF], F32)
         gates = {}
         grouped_x = {}
 
@@ -195,56 +211,79 @@ def tile_share_lstm_cell_pa_kernel(
             grouped_x[t] = grouped
 
         def quantize_x(t):
-            group, place = home[t]
             for g in range(PASSES):
                 nc.vector.quantize_mx(
-                    out=x_codes[group][:, g, place * P : (place + 1) * P].bitcast(FP8X4),
-                    scales=x_scales[group][:, g, place * P : (place + 1) * P],
+                    out=x_codes[:, 0, g, t * P : (t + 1) * P].bitcast(FP8X4),
+                    scales=x_scales[:, 0, g, t * P : (t + 1) * P],
                     in_=grouped_x[t][:, g, :, :].rearrange("p r k -> p (r k)"),
                 )
 
-        def transpose_states(t, pool, tag):
+        def split_x_quads(g, copy):
+            parted = stage.tile([P, 2, HALF // QUAD, QUAD], F32, align_bytes=64)
+            copy(
+                out=parted[:],
+                in_=x_quads[:, g, :, :].bitcast(F32).rearrange("p b (i u) -> p u b i", u=2),
+            )
+            return parted
+
+        def turn_x_quads(parted):
+            turned = stage.tile([P, 2, HALF], F32, align_bytes=64)
+            nc.vector.transpose(turned[:].rearrange("p u r -> p (u r)"), parted[:].rearrange("p u b i -> p (u b i)"))
+            return turned
+
+        def group_x_quads(turned, copy):
+            grouped = stage.tile([P, HALF, 4], BF16, align_bytes=64)
+            copy(out=grouped[:].rearrange("p r k -> p (r k)").bitcast(F32).rearrange("p (r u) -> p r u", u=2), in_=turned[:].rearrange("p u r -> p r u"))
+            return grouped
+
+        def quantize_x_quads(g, grouped):
+            nc.vector.quantize_mx(
+                out=x_codes[:, 1, g, :].bitcast(FP8X4),
+                scales=x_scales[:, 1, g, :],
+                in_=grouped[:].rearrange("p r k -> p (r k)"),
+            )
+
+        def transpose_states(t, copy, pool, tag):
             st_ps = pool.tile([P, 4, P], F32, tag=tag)
             for j in range(4):
                 nc.tensor.transpose(st_ps[:, j, :], state_sb[j][:, t, :].bitcast(F32), ident[:])
-            nc.scalar.copy(out=states_t_sb[:, t, :, :], in_=st_ps[:])
+            copy(out=states_t_first[:, t, :, :], in_=st_ps[:])
 
-        def mx_product(group, blocks, pool, tag):
-            rows = len(MX_GROUPS[group]) * P
-            acc = pool.tile([P, BANK // rows, rows], F32, tag=tag)
-            for n, j in enumerate(blocks):
-                for g in range(PASSES):
-                    nc.tensor.matmul_mx(
-                        out=acc[:, n, :],
-                        lhsT=w_words[:, j // HALF_BLOCKS, g, 2 * P * (j % HALF_BLOCKS) : 2 * P * (j % HALF_BLOCKS + 1)].bitcast(FP4X4),
-                        lhsT_scale=w_scales[:, g, P * j : P * (j + 1)],
-                        rhs=x_codes[group][:, g, :].bitcast(FP8X4),
-                        rhs_scale=x_scales[group][:, g, :],
-                        start=(g == 0),
-                        stop=(g == PASSES - 1),
-                    )
+        def turn_state_quads(j):
+            nc.vector.transpose(
+                states_t_second[:, j, :], state_quads[j][:].rearrange("p b w -> p (b w)").bitcast(F32)
+            )
+
+        def mx_product(half, j, pool, tag):
+            acc = pool.tile([P, HALF], F32, tag=tag)
+            for g in range(PASSES):
+                nc.tensor.matmul_mx(
+                    out=acc[:],
+                    lhsT=w_words[:, j // HALF_BLOCKS, g, 2 * P * (j % HALF_BLOCKS) : 2 * P * (j % HALF_BLOCKS + 1)].bitcast(
+                        FP4X4
+                    ),
+                    lhsT_scale=w_scales[:, g, P * j : P * (j + 1)],
+                    rhs=x_codes[:, half, g, :].bitcast(FP8X4),
+                    rhs_scale=x_scales[:, half, g, :],
+                    start=(g == 0),
+                    stop=(g == PASSES - 1),
+                )
             return acc
 
-        def mx_copy(group, blocks, acc, on_vector):
-            first, count = blocks[0], len(blocks)
-            rows = len(MX_GROUPS[group]) * P
+        def mx_copy(half, j, acc, on_vector):
             if on_vector:
-                nc.vector.tensor_tensor(
-                    out=mx_sb[group][:, first : first + count, :],
-                    in0=acc[:, 0:count, :],
-                    in1=bias_col[:, first : first + count].unsqueeze(2).to_broadcast([P, count, rows]),
-                    op=ALU.add,
+                nc.vector.tensor_scalar(
+                    out=mx_sb[:, half, j, :], in0=acc[:], scalar1=bias_col[:, j : j + 1], scalar2=None, op0=ALU.add
                 )
             else:
-                for n, j in enumerate(blocks):
-                    nc.scalar.activation(
-                        out=mx_sb[group][:, j, :], in_=acc[:, n, :], func=ACT.Identity, bias=bias_col[:, j : j + 1]
-                    )
+                nc.scalar.activation(out=mx_sb[:, half, j, :], in_=acc[:], func=ACT.Identity, bias=bias_col[:, j : j + 1])
 
         sums = {}
 
         def plain_product(t):
-            states_t = states_t_sb[:, t, :, :].bitcast(BF16).rearrange("p j (r e) -> p j r e", e=2)
+            half, place = divmod(t, TILES_HALF)
+            words = states_t_first[:, place, :, :] if half == 0 else states_t_second[:, :, place * P : (place + 1) * P]
+            states_t = words.bitcast(BF16).rearrange("p j (r e) -> p j r e", e=2)
             sums[t] = []
             for c0 in range(0, GATES, BANK):
                 width = min(BANK, GATES - c0)
@@ -263,13 +302,13 @@ def tile_share_lstm_cell_pa_kernel(
                         )
 
         def add_mx(t):
-            group, place = home[t]
+            half, place = divmod(t, TILES_HALF)
             for bank, c0 in enumerate(range(0, GATES, BANK)):
                 blocks = range(c0 // P, min(c0 + BANK, GATES) // P)
                 for j in blocks:
                     nc.tensor.matmul(
                         sums[t][bank][:, j * P - c0 : (j + 1) * P - c0],
-                        lhsT=mx_sb[group][:, j, place * P : (place + 1) * P],
+                        lhsT=mx_sb[:, half, j, place * P : (place + 1) * P],
                         rhs=ident[:],
                         is_transpose=True,
                         start=False,
@@ -288,7 +327,7 @@ def tile_share_lstm_cell_pa_kernel(
                 else:
                     nc.scalar.activation(out=gate[:, c0 : c0 + width], in_=total[:, 0:width], func=ACT.Sigmoid)
 
-        out_views = [o.rearrange("(p t) d -> p t d", t=TILES) for o in (out_0, out_1, out_2, out_3, out_4)]
+        out_views = [o.rearrange("(t p) d -> p t d", p=P) for o in (out_0, out_1, out_2, out_3, out_4)]
 
         def fused(out, in0, scalar, in1, op0, op1):
             nc.vector.scalar_tensor_tensor(out=out, in0=in0, scalar=scalar, in1=in1, op0=op0, op1=op1)
@@ -375,63 +414,63 @@ def tile_share_lstm_cell_pa_kernel(
                 nc.tensor.matmul(idle_ps[:], lhsT=idle_sb[:, 0:P], rhs=idle_sb[:], start=True, stop=True)
 
         SUM, MX, TR = (psum_sum, "sum"), (psum_mx, "mx"), (psum_tr, "tr")
-        SUM, MX, TR = (psum_sum, "sum"), (psum_mx, "mx"), (psum_tr, "tr")
         keep_busy(4)
         transpose_x(0, nc.scalar.copy, *SUM)
+        transpose_x(1, nc.vector.tensor_copy, *SUM)
         quantize_x(0)
-        keep_busy(2)
-        transpose_weights(0, 4, nc.scalar.copy)
-        transpose_weights(4, 8, nc.scalar.copy)
-        transpose_bias()
-        keep_busy(2)
-        for n, blocks in enumerate(((0, 1, 2, 3), (4, 5, 6), (7, 8, 9, 10), (11, 12, 13))):
-            acc = mx_product(0, blocks, *MX)
-            mx_copy(0, blocks, acc, n % 2 == 0)
-        transpose_states(0, *SUM)
-        transpose_states(1, *TR)
-        transpose_weights(8, 12, nc.vector.tensor_copy)
-        transpose_weights(12, 14, nc.vector.tensor_copy)
-        transpose_x(1, nc.scalar.copy, *MX)
-        transpose_x(2, nc.vector.tensor_copy, *MX)
         quantize_x(1)
+        transpose_weights(0, 4, nc.scalar.copy)
+        transpose_weights(4, 8, nc.vector.tensor_copy)
+        keep_busy(2)
+        transpose_x(2, nc.scalar.copy, *MX)
+        transpose_x(3, nc.vector.tensor_copy, *MX)
         quantize_x(2)
-        plain_product(0)
-        transpose_x(3, nc.scalar.copy, *MX)
-        transpose_x(4, nc.vector.tensor_copy, *TR)
         quantize_x(3)
-        quantize_x(4)
-        prepare_factors()
+        transpose_weights(8, 12, nc.scalar.copy)
+        transpose_weights(12, 14, nc.scalar.copy)
+        keep_busy(2)
+        accs = []
+        for j in range(GATE_TILES):
+            accs.append(mx_product(0, j, *(MX if j % 2 == 0 else SUM)))
+            if j == 2:
+                transpose_bias()
+                for n in range(3):
+                    mx_copy(0, n, accs[n], n % 2 == 0)
+                prepare_factors()
+            if j > 2:
+                mx_copy(0, j, accs[j], j % 2 == 0 and j < 8)
+            if j == 9:
+                transpose_states(0, nc.vector.tensor_copy, *SUM)
+                transpose_states(1, nc.scalar.copy, *TR)
+        transpose_states(2, nc.scalar.copy, *MX)
+        transpose_states(3, nc.scalar.copy, *MX)
+        parted = [split_x_quads(g, nc.vector.tensor_copy) for g in range(PASSES)]
+        turned = [turn_x_quads(p) for p in parted]
+        grouped = [group_x_quads(p, nc.vector.tensor_copy) for p in turned]
+        for g in range(PASSES):
+            quantize_x_quads(g, grouped[g])
+        for j in range(4):
+            turn_state_quads(j)
+        plain_product(0)
         for t in range(TILES):
             add_mx(t)
             activate(t)
             kept, new, c_t, tanh, b_o = cell_steps(t)
-            if t in X_STEPS:
-                transpose_x(X_STEPS[t], nc.scalar.copy, *TR)
+            early, late = [kept, new], [b_o, c_t, tanh]
             if t:
                 s_0, h_t, r_1, s_1, p_2, r_2, s_2 = share_steps(t - 1, slice(0, DH), True)
-                early = (s_0, h_t, r_1)
+                early, late = [s_0, h_t, r_1, kept, p_2, new, s_1], [c_t, tanh, r_2, b_o, s_2]
+            if t:
                 for step in early:
                     step()
-            kept()
-            for n, (group, blocks) in enumerate(MX_STEPS[t]):
-                acc = mx_product(group, blocks, *MX)
-                mx_copy(group, blocks, acc, n < 4 or n % 2 == 0 if t == 0 else n < 1 and t < 4)
-                if n == (5 if t == 0 else 0):
-                    new()
-            if not MX_STEPS[t]:
-                new()
-            c_t()
-            tanh()
-            if t:
-                s_1()
-            b_o()
-            if t:
-                for step in (p_2, r_2, s_2):
+            for n, j in enumerate(MX_CHUNKS[t]):
+                acc = mx_product(1, j, *MX)
+                mx_copy(1, j, acc, n == 0)
+            if t == 0:
+                for step in early:
                     step()
-            if t in X_STEPS:
-                quantize_x(X_STEPS[t])
-            if t + 2 < TILES:
-                transpose_states(t + 2, *MX)
+            for step in late:
+                step()
             if t + 1 < TILES:
                 plain_product(t + 1)
         left = share_steps(TILES - 1, slice(0, DH // 2), False)

@@ -29,7 +29,7 @@ K_PASS = 4 * P
 PASSES = DI // K_PASS
 BANK = 512
 
-MX_CHUNKS = ((0, 1, 2, 3), (4, 5, 6, 7), (8, 9, 10), (11, 12, 13), (), (), (), ())
+MX_CHUNKS = ((0, 1), (2, 3), (4, 5), (6, 7), (), (), (), ())
 QUAD = 32
 
 FLOPS = 2 * ROWS * GATES * (DI + DH)
@@ -142,6 +142,8 @@ def tile_share_lstm_cell_pa_kernel(
         load_states(0, 2)
         load_x_quads()
         load_states(2, 4)
+        c_sb = keep.tile([P, TILES, DH], BF16)
+        nc.sync.dma_start(out=c_sb[:], in_=c_minors.rearrange("(t p) d -> p t d", p=P))
         load_state_quads()
 
         ident = keep.tile([P, P], F32)
@@ -153,8 +155,6 @@ def tile_share_lstm_cell_pa_kernel(
             wsh_sb = keep.tile([P, DH // P, DH], BF16, name="wsh_sb%d" % i)
             nc.gpsimd.dma_start(out=wsh_sb[:], in_=weight_sh.rearrange("(j p) k -> p j k", p=P))
             weight_row_tiles.extend([wsh_sb[:, j, :] for j in range(DH // P)])
-        c_sb = keep.tile([P, TILES, DH], BF16)
-        nc.gpsimd.dma_start(out=c_sb[:], in_=c_minors.rearrange("(t p) d -> p t d", p=P))
 
         bias_rows = keep.tile([P, P], F32)
         columns = keep.tile([P, GATE_TILES + TILES], F32)
@@ -270,6 +270,33 @@ def tile_share_lstm_cell_pa_kernel(
                 )
             return acc
 
+        def mx_product_tile(t, blocks, pool, tag):
+            half, place = divmod(t, TILES_HALF)
+            rows = slice(place * P, (place + 1) * P)
+            acc = pool.tile([P, BANK // P, P], F32, tag=tag)
+            for n, j in enumerate(blocks):
+                for g in range(PASSES):
+                    nc.tensor.matmul_mx(
+                        out=acc[:, n, :],
+                        lhsT=w_words[:, j // HALF_BLOCKS, g, 2 * P * (j % HALF_BLOCKS) : 2 * P * (j % HALF_BLOCKS + 1)].bitcast(
+                            FP4X4
+                        ),
+                        lhsT_scale=w_scales[:, g, P * j : P * (j + 1)],
+                        rhs=x_codes[:, half, g, rows].bitcast(FP8X4),
+                        rhs_scale=x_scales[:, half, g, rows],
+                        start=(g == 0),
+                        stop=(g == PASSES - 1),
+                    )
+            return acc
+
+        def mx_copy_tile(t, blocks, acc):
+            half, place = divmod(t, TILES_HALF)
+            rows = slice(place * P, (place + 1) * P)
+            for n, j in enumerate(blocks):
+                nc.scalar.activation(
+                    out=mx_sb[:, half, j, rows], in_=acc[:, n, :], func=ACT.Identity, bias=bias_col[:, j : j + 1]
+                )
+
         def mx_copy(half, j, acc, on_vector):
             if on_vector:
                 nc.vector.tensor_scalar(
@@ -280,15 +307,15 @@ def tile_share_lstm_cell_pa_kernel(
 
         sums = {}
 
-        def plain_product(t):
+        def gate_sums(t, banks):
             half, place = divmod(t, TILES_HALF)
             words = states_t_first[:, place, :, :] if half == 0 else states_t_second[:, :, place * P : (place + 1) * P]
             states_t = words.bitcast(BF16).rearrange("p j (r e) -> p j r e", e=2)
-            sums[t] = []
-            for c0 in range(0, GATES, BANK):
+            for bank in banks:
+                c0 = bank * BANK
                 width = min(BANK, GATES - c0)
                 total = psum_sum.tile([P, BANK], F32, tag="sum")
-                sums[t].append(total)
+                sums[t, bank] = total
                 step = BANK if c0 < LSTM else DH
                 for b0 in range(c0, c0 + width, step):
                     source = max(0, b0 // DH - 3)
@@ -300,14 +327,12 @@ def tile_share_lstm_cell_pa_kernel(
                             start=(b0 == c0 and e == 0),
                             stop=False,
                         )
-
-        def add_mx(t):
-            half, place = divmod(t, TILES_HALF)
-            for bank, c0 in enumerate(range(0, GATES, BANK)):
+            for bank in banks:
+                c0 = bank * BANK
                 blocks = range(c0 // P, min(c0 + BANK, GATES) // P)
                 for j in blocks:
                     nc.tensor.matmul(
-                        sums[t][bank][:, j * P - c0 : (j + 1) * P - c0],
+                        sums[t, bank][:, j * P - c0 : (j + 1) * P - c0],
                         lhsT=mx_sb[:, half, j, place * P : (place + 1) * P],
                         rhs=ident[:],
                         is_transpose=True,
@@ -315,12 +340,14 @@ def tile_share_lstm_cell_pa_kernel(
                         stop=(j == blocks[-1]),
                     )
 
-        def activate(t):
-            gate = chain.tile([P, GATES], F32)
-            gates[t] = gate
-            for bank, c0 in enumerate(range(0, GATES, BANK)):
+        def activate(t, banks):
+            if 0 in banks:
+                gates[t] = chain.tile([P, GATES], F32, name="gate")
+            gate = gates[t]
+            for bank in banks:
+                c0 = bank * BANK
                 width = min(BANK, GATES - c0)
-                total = sums[t][bank]
+                total = sums[t, bank]
                 if c0 == 2 * DH:
                     nc.scalar.activation(out=gate[:, c0 : c0 + DH], in_=total[:, 0:DH], func=ACT.Sigmoid)
                     nc.scalar.activation(out=gate[:, c0 + DH : c0 + BANK], in_=total[:, DH:BANK], func=ACT.Tanh)
@@ -449,30 +476,33 @@ def tile_share_lstm_cell_pa_kernel(
         grouped = [group_x_quads(p, nc.vector.tensor_copy) for p in turned]
         for g in range(PASSES):
             quantize_x_quads(g, grouped[g])
-        for j in range(4):
-            turn_state_quads(j)
-        plain_product(0)
         for t in range(TILES):
-            add_mx(t)
-            activate(t)
+            gate_sums(t, (0, 1))
+            activate(t, (0, 1))
+            gate_sums(t, (2, 3))
+            activate(t, (2, 3))
             kept, new, c_t, tanh, b_o = cell_steps(t)
             early, late = [kept, new], [b_o, c_t, tanh]
             if t:
                 s_0, h_t, r_1, s_1, p_2, r_2, s_2 = share_steps(t - 1, slice(0, DH), True)
                 early, late = [s_0, h_t, r_1, kept, p_2, new, s_1], [c_t, tanh, r_2, b_o, s_2]
-            if t:
                 for step in early:
                     step()
             for n, j in enumerate(MX_CHUNKS[t]):
                 acc = mx_product(1, j, *MX)
-                mx_copy(1, j, acc, n == 0)
+                mx_copy(1, j, acc, t == 0 and n == 0)
+            if TILES_HALF <= t + 1 < TILES:
+                for blocks in ((8, 9, 10, 11), (12, 13)):
+                    acc = mx_product_tile(t + 1, blocks, *MX)
+                    mx_copy_tile(t + 1, blocks, acc)
             if t == 0:
                 for step in early:
                     step()
             for step in late:
                 step()
-            if t + 1 < TILES:
-                plain_product(t + 1)
+            if t in (1, 2):
+                turn_state_quads(2 * t - 2)
+                turn_state_quads(2 * t - 1)
         left = share_steps(TILES - 1, slice(0, DH // 2), False)
         right = share_steps(TILES - 1, slice(DH // 2, DH), True)
         for a, b in zip(left, right):

@@ -29,7 +29,7 @@ K_PASS = 4 * P
 PASSES = DI // K_PASS
 BANK = 512
 
-MX_CHUNKS = ((0, 1), (2, 3), (4, 5), (6, 7), (), (), (), ())
+MX_CHUNKS = ((), (0, 1, 2), (3, 4, 5), (6, 7), (), (), (), ())
 QUAD = 32
 
 FLOPS = 2 * ROWS * GATES * (DI + DH)
@@ -161,8 +161,10 @@ def tile_share_lstm_cell_pa_kernel(
         bias_col = columns[:, 0:GATE_TILES]
         factors = keep.tile([P, 3, TILES], F32)
 
-        def transpose_bias():
+        def sum_bias():
             nc.vector.tensor_tensor(out=bias_rows[:], in0=bias_x_rows[:], in1=bias_s_rows[:], op=ALU.add)
+
+        def transpose_bias():
             bias_ps = psum_tr.tile([P, 4, P], F32, tag="tr")
             nc.tensor.transpose(bias_ps[:, 0, :], bias_rows[:], ident[:])
             nc.vector.tensor_copy(out=columns[:], in_=bias_ps[:, 0, 0 : GATE_TILES + TILES])
@@ -307,38 +309,39 @@ def tile_share_lstm_cell_pa_kernel(
 
         sums = {}
 
-        def gate_sums(t, banks):
+        def plain_product(t, bank):
             half, place = divmod(t, TILES_HALF)
             words = states_t_first[:, place, :, :] if half == 0 else states_t_second[:, :, place * P : (place + 1) * P]
             states_t = words.bitcast(BF16).rearrange("p j (r e) -> p j r e", e=2)
-            for bank in banks:
-                c0 = bank * BANK
-                width = min(BANK, GATES - c0)
-                total = psum_sum.tile([P, BANK], F32, tag="sum")
-                sums[t, bank] = total
-                step = BANK if c0 < LSTM else DH
-                for b0 in range(c0, c0 + width, step):
-                    source = max(0, b0 // DH - 3)
-                    for e in range(2):
-                        nc.tensor.matmul(
-                            total[:, b0 - c0 : b0 - c0 + step],
-                            lhsT=states_t[:, source, :, e],
-                            rhs=w_t_halves[:, b0 : b0 + step, e],
-                            start=(b0 == c0 and e == 0),
-                            stop=False,
-                        )
-            for bank in banks:
-                c0 = bank * BANK
-                blocks = range(c0 // P, min(c0 + BANK, GATES) // P)
-                for j in blocks:
+            c0 = bank * BANK
+            width = min(BANK, GATES - c0)
+            total = psum_sum.tile([P, BANK], F32, tag="sum")
+            sums[t, bank] = total
+            step = BANK if c0 < LSTM else DH
+            for b0 in range(c0, c0 + width, step):
+                source = max(0, b0 // DH - 3)
+                for e in range(2):
                     nc.tensor.matmul(
-                        sums[t, bank][:, j * P - c0 : (j + 1) * P - c0],
-                        lhsT=mx_sb[:, half, j, place * P : (place + 1) * P],
-                        rhs=ident[:],
-                        is_transpose=True,
-                        start=False,
-                        stop=(j == blocks[-1]),
+                        total[:, b0 - c0 : b0 - c0 + step],
+                        lhsT=states_t[:, source, :, e],
+                        rhs=w_t_halves[:, b0 : b0 + step, e],
+                        start=(b0 == c0 and e == 0),
+                        stop=False,
                     )
+
+        def add_mx(t, bank):
+            half, place = divmod(t, TILES_HALF)
+            c0 = bank * BANK
+            blocks = range(c0 // P, min(c0 + BANK, GATES) // P)
+            for j in blocks:
+                nc.tensor.matmul(
+                    sums[t, bank][:, j * P - c0 : (j + 1) * P - c0],
+                    lhsT=mx_sb[:, half, j, place * P : (place + 1) * P],
+                    rhs=ident[:],
+                    is_transpose=True,
+                    start=False,
+                    stop=(j == blocks[-1]),
+                )
 
         def activate(t, banks):
             if 0 in banks:
@@ -450,56 +453,55 @@ def tile_share_lstm_cell_pa_kernel(
         transpose_weights(4, 8, nc.vector.tensor_copy)
         keep_busy(2)
         transpose_x(2, nc.scalar.copy, *MX)
+        sum_bias()
         transpose_x(3, nc.vector.tensor_copy, *MX)
         quantize_x(2)
         quantize_x(3)
         transpose_weights(8, 12, nc.scalar.copy)
         transpose_weights(12, 14, nc.scalar.copy)
+        transpose_bias()
+        prepare_factors()
         keep_busy(2)
-        accs = []
         for j in range(GATE_TILES):
-            accs.append(mx_product(0, j, *(MX if j % 2 == 0 else SUM)))
-            if j == 2:
-                transpose_bias()
-                for n in range(3):
-                    mx_copy(0, n, accs[n], n % 2 == 0)
-                prepare_factors()
-            if j > 2:
-                mx_copy(0, j, accs[j], j % 2 == 0 and j < 8)
-            if j == 9:
-                transpose_states(0, nc.vector.tensor_copy, *SUM)
-                transpose_states(1, nc.scalar.copy, *TR)
+            acc = mx_product(0, j, *(MX if j % 2 == 0 else SUM))
+            mx_copy(0, j, acc, j % 2 == 0 and j < 8)
+        transpose_states(0, nc.scalar.copy, *MX)
+        transpose_states(1, nc.scalar.copy, *MX)
         transpose_states(2, nc.scalar.copy, *MX)
-        transpose_states(3, nc.scalar.copy, *MX)
+        transpose_states(3, nc.scalar.copy, *TR)
         parted = [split_x_quads(g, nc.vector.tensor_copy) for g in range(PASSES)]
         turned = [turn_x_quads(p) for p in parted]
         grouped = [group_x_quads(p, nc.vector.tensor_copy) for p in turned]
         for g in range(PASSES):
             quantize_x_quads(g, grouped[g])
+        plain_product(0, 0)
         for t in range(TILES):
-            gate_sums(t, (0, 1))
-            activate(t, (0, 1))
-            gate_sums(t, (2, 3))
-            activate(t, (2, 3))
-            kept, new, c_t, tanh, b_o = cell_steps(t)
-            early, late = [kept, new], [b_o, c_t, tanh]
-            if t:
-                s_0, h_t, r_1, s_1, p_2, r_2, s_2 = share_steps(t - 1, slice(0, DH), True)
-                early, late = [s_0, h_t, r_1, kept, p_2, new, s_1], [c_t, tanh, r_2, b_o, s_2]
-                for step in early:
-                    step()
             for n, j in enumerate(MX_CHUNKS[t]):
                 acc = mx_product(1, j, *MX)
-                mx_copy(1, j, acc, t == 0 and n == 0)
-            if TILES_HALF <= t + 1 < TILES:
+                mx_copy(1, j, acc, False)
+            if t >= TILES_HALF:
                 for blocks in ((8, 9, 10, 11), (12, 13)):
-                    acc = mx_product_tile(t + 1, blocks, *MX)
-                    mx_copy_tile(t + 1, blocks, acc)
-            if t == 0:
-                for step in early:
-                    step()
-            for step in late:
+                    acc = mx_product_tile(t, blocks, *MX)
+                    mx_copy_tile(t, blocks, acc)
+            plain_product(t, 1)
+            add_mx(t, 0)
+            add_mx(t, 1)
+            activate(t, (0, 1))
+            plain_product(t, 2)
+            plain_product(t, 3)
+            add_mx(t, 2)
+            add_mx(t, 3)
+            activate(t, (2, 3))
+            if t + 1 < TILES:
+                plain_product(t + 1, 0)
+            kept, new, c_t, tanh, b_o = cell_steps(t)
+            order = [kept, new, b_o, c_t]
+            if t:
+                s_0, h_t, r_1, s_1, p_2, r_2, s_2 = share_steps(t - 1, slice(0, DH), True)
+                order = [s_0, h_t, r_1, kept, p_2, new, s_1, c_t, r_2, b_o, s_2]
+            for step in order:
                 step()
+            tanh()
             if t in (1, 2):
                 turn_state_quads(2 * t - 2)
                 turn_state_quads(2 * t - 1)

@@ -29,7 +29,7 @@ K_PASS = 4 * P
 PASSES = DI // K_PASS
 BANK = 512
 
-MX_CHUNKS = ((), (0, 1, 2), (3, 4, 5), (6, 7), (), (), (), ())
+MX_CHUNKS = ((), (0, 1, 2), (3, 4, 5), (6, 7, 8, 9), (), (), (), ())
 QUAD = 32
 
 FLOPS = 2 * ROWS * GATES * (DI + DH)
@@ -89,9 +89,8 @@ def tile_share_lstm_cell_pa_kernel(
         x_view = x.rearrange("(t p) k -> p t k", p=P)
         states = (h_minors, s0, s1, s2)
         state_views = [s.rearrange("(t p) d -> p t d", p=P) for s in states]
-        state_sb = [keep.tile([P, TILES_HALF, DH], BF16, name="state_sb%d" % j) for j in range(4)]
+        state_sb = [keep.tile([P, TILES, DH], BF16, name="state_sb%d" % j) for j in range(4)]
         x_quads = keep.tile([P, PASSES, HALF // QUAD, P], BF16, align_bytes=64)
-        state_quads = [keep.tile([P, HALF // QUAD, DH // 4], BF16, align_bytes=64, name="state_quads%d" % j) for j in range(4)]
 
         def load_x(first, last):
             nc.sync.dma_start(out=x_sb[:, first:last, :], in_=x_view[:, first:last, :])
@@ -105,12 +104,6 @@ def tile_share_lstm_cell_pa_kernel(
             for g in range(PASSES):
                 for r in range(4):
                     nc.sync.dma_start(out=x_quads[QUAD * r : QUAD * (r + 1), g, :, :], in_=view[g, r])
-
-        def load_state_quads():
-            for n in range(4):
-                view = states[n][HALF:ROWS, :].rearrange("(b j) (r w) -> r j b w", j=QUAD, r=4)
-                for r in range(4):
-                    nc.sync.dma_start(out=state_quads[n][QUAD * r : QUAD * (r + 1), :, :], in_=view[r])
 
         load_x(0, 1)
         load_x(1, 2)
@@ -144,7 +137,7 @@ def tile_share_lstm_cell_pa_kernel(
         load_states(2, 4)
         c_sb = keep.tile([P, TILES, DH], BF16)
         nc.sync.dma_start(out=c_sb[:], in_=c_minors.rearrange("(t p) d -> p t d", p=P))
-        load_state_quads()
+        load_states(4, TILES)
 
         ident = keep.tile([P, P], F32)
         make_identity(nc, ident[:])
@@ -194,8 +187,7 @@ def tile_share_lstm_cell_pa_kernel(
 
         x_codes = keep.tile([P, HALVES, PASSES, HALF], U32, align_bytes=64)
         x_scales = keep.tile([P, HALVES, PASSES, HALF], U8, align_bytes=64)
-        states_t_first = keep.tile([P, TILES_HALF, 4, P], F32)
-        states_t_second = keep.tile([P, 4, HALF], F32, align_bytes=64)
+        states_t_sb = keep.tile([P, TILES, 4, P], F32)
         mx_sb = keep.tile([P, HALVES, GATE_TILES, HALF], F32)
         gates = {}
         grouped_x = {}
@@ -249,12 +241,7 @@ def tile_share_lstm_cell_pa_kernel(
             st_ps = pool.tile([P, 4, P], F32, tag=tag)
             for j in range(4):
                 nc.tensor.transpose(st_ps[:, j, :], state_sb[j][:, t, :].bitcast(F32), ident[:])
-            copy(out=states_t_first[:, t, :, :], in_=st_ps[:])
-
-        def turn_state_quads(j):
-            nc.vector.transpose(
-                states_t_second[:, j, :], state_quads[j][:].rearrange("p b w -> p (b w)").bitcast(F32)
-            )
+            copy(out=states_t_sb[:, t, :, :], in_=st_ps[:])
 
         def mx_product(half, j, pool, tag):
             acc = pool.tile([P, HALF], F32, tag=tag)
@@ -310,9 +297,7 @@ def tile_share_lstm_cell_pa_kernel(
         sums = {}
 
         def plain_product(t, bank):
-            half, place = divmod(t, TILES_HALF)
-            words = states_t_first[:, place, :, :] if half == 0 else states_t_second[:, :, place * P : (place + 1) * P]
-            states_t = words.bitcast(BF16).rearrange("p j (r e) -> p j r e", e=2)
+            states_t = states_t_sb[:, t, :, :].bitcast(BF16).rearrange("p j (r e) -> p j r e", e=2)
             c0 = bank * BANK
             width = min(BANK, GATES - c0)
             total = psum_sum.tile([P, BANK], F32, tag="sum")
@@ -449,9 +434,9 @@ def tile_share_lstm_cell_pa_kernel(
         transpose_x(1, nc.vector.tensor_copy, *SUM)
         quantize_x(0)
         quantize_x(1)
+        keep_busy(2)
         transpose_weights(0, 4, nc.scalar.copy)
         transpose_weights(4, 8, nc.vector.tensor_copy)
-        keep_busy(2)
         transpose_x(2, nc.scalar.copy, *MX)
         sum_bias()
         transpose_x(3, nc.vector.tensor_copy, *MX)
@@ -480,9 +465,8 @@ def tile_share_lstm_cell_pa_kernel(
                 acc = mx_product(1, j, *MX)
                 mx_copy(1, j, acc, False)
             if t >= TILES_HALF:
-                for blocks in ((8, 9, 10, 11), (12, 13)):
-                    acc = mx_product_tile(t, blocks, *MX)
-                    mx_copy_tile(t, blocks, acc)
+                acc = mx_product_tile(t, (10, 11, 12, 13), *MX)
+                mx_copy_tile(t, (10, 11, 12, 13), acc)
             plain_product(t, 1)
             add_mx(t, 0)
             add_mx(t, 1)
@@ -492,6 +476,8 @@ def tile_share_lstm_cell_pa_kernel(
             add_mx(t, 2)
             add_mx(t, 3)
             activate(t, (2, 3))
+            if 2 <= t < TILES_HALF + 2:
+                transpose_states(t + 2, nc.scalar.copy, *TR)
             if t + 1 < TILES:
                 plain_product(t + 1, 0)
             kept, new, c_t, tanh, b_o = cell_steps(t)
@@ -502,9 +488,6 @@ def tile_share_lstm_cell_pa_kernel(
             for step in order:
                 step()
             tanh()
-            if t in (1, 2):
-                turn_state_quads(2 * t - 2)
-                turn_state_quads(2 * t - 1)
         left = share_steps(TILES - 1, slice(0, DH // 2), False)
         right = share_steps(TILES - 1, slice(DH // 2, DH), True)
         for a, b in zip(left, right):

@@ -435,15 +435,13 @@ def tile_share_lstm_cell_pa_kernel(
         quantize_x(0)
         quantize_x(1)
         keep_busy(2)
-        transpose_weights(0, 4, nc.scalar.copy)
-        transpose_weights(4, 8, nc.vector.tensor_copy)
         transpose_x(2, nc.scalar.copy, *MX)
         sum_bias()
         transpose_x(3, nc.vector.tensor_copy, *MX)
         quantize_x(2)
         quantize_x(3)
-        transpose_weights(8, 12, nc.scalar.copy)
-        transpose_weights(12, 14, nc.scalar.copy)
+        transpose_weights(0, 4, nc.scalar.copy)
+        transpose_weights(4, 8, nc.scalar.copy)
         transpose_bias()
         prepare_factors()
         keep_busy(2)
@@ -451,6 +449,8 @@ def tile_share_lstm_cell_pa_kernel(
             acc = mx_product(0, j, *(MX if j % 2 == 0 else SUM))
             mx_copy(0, j, acc, j % 2 == 0 and j < 8)
         transpose_states(0, nc.scalar.copy, *MX)
+        transpose_weights(8, 12, nc.scalar.copy)
+        transpose_weights(12, 14, nc.scalar.copy)
         transpose_states(1, nc.scalar.copy, *MX)
         transpose_states(2, nc.scalar.copy, *MX)
         transpose_states(3, nc.scalar.copy, *TR)
@@ -460,13 +460,18 @@ def tile_share_lstm_cell_pa_kernel(
         for g in range(PASSES):
             quantize_x_quads(g, grouped[g])
         plain_product(0, 0)
+        tanh_of = {}
         for t in range(TILES):
             for n, j in enumerate(MX_CHUNKS[t]):
+                if n == 2:
+                    tanh_of[t - 1]()
                 acc = mx_product(1, j, *MX)
                 mx_copy(1, j, acc, False)
             if t >= TILES_HALF:
                 acc = mx_product_tile(t, (10, 11, 12, 13), *MX)
                 mx_copy_tile(t, (10, 11, 12, 13), acc)
+            if t and not MX_CHUNKS[t]:
+                tanh_of[t - 1]()
             plain_product(t, 1)
             add_mx(t, 0)
             add_mx(t, 1)
@@ -487,7 +492,8 @@ def tile_share_lstm_cell_pa_kernel(
                 order = [s_0, h_t, r_1, kept, p_2, new, s_1, c_t, r_2, b_o, s_2]
             for step in order:
                 step()
-            tanh()
+            tanh_of[t] = tanh
+        tanh_of[TILES - 1]()
         left = share_steps(TILES - 1, slice(0, DH // 2), False)
         right = share_steps(TILES - 1, slice(DH // 2, DH), True)
         for a, b in zip(left, right):

@@ -29,7 +29,7 @@ K_PASS = 4 * P
 PASSES = DI // K_PASS
 BANK = 512
 
-MX_CHUNKS = ((), (0, 1, 2), (3, 4, 5), (6, 7, 8, 9), (), (), (), ())
+MX_CHUNKS = ((), (0, 1, 2), (3, 4, 5), (), (), (), (), ())
 QUAD = 32
 
 FLOPS = 2 * ROWS * GATES * (DI + DH)
@@ -357,7 +357,8 @@ def tile_share_lstm_cell_pa_kernel(
             new = temps.tile([P, DH], F32)
             tanh_c = temps.tile([P, DH], F32)
             b_o = temps.tile([P, 3, DH], F32)
-            work[t] = (res, tanh_c, b_o)
+            rests = [temps.tile([P, DH], F32, name="rest%d" % n) for n in range(3)]
+            work[t] = (res, tanh_c, b_o, rests)
             o_g = gate[:, 2 * DH : 3 * DH]
             b_g = gate[:, LSTM:GATES].rearrange("p (j d) -> p j d", j=3)
 
@@ -380,13 +381,10 @@ def tile_share_lstm_cell_pa_kernel(
             return step_kept, step_new, step_c, step_tanh, step_b
 
         def share_steps(t, cols, stores):
-            res, tanh_c_all, b_o = work[t]
+            res, tanh_c_all, b_o, (rest1, part2, rest2) = work[t]
             tanh_c = tanh_c_all[:, cols]
             m1, m2, m3 = [factors[:, n, t : t + 1] for n in range(3)]
             o_g = gates[t][:, 2 * DH + cols.start : 2 * DH + cols.stop]
-            rest1 = temps.tile([P, DH], F32)
-            part2 = temps.tile([P, DH], F32)
-            rest2 = temps.tile([P, DH], F32)
 
             def store(k):
                 if stores:
@@ -463,14 +461,17 @@ def tile_share_lstm_cell_pa_kernel(
         tanh_of = {}
         for t in range(TILES):
             for n, j in enumerate(MX_CHUNKS[t]):
-                if n == 2:
-                    tanh_of[t - 1]()
                 acc = mx_product(1, j, *MX)
                 mx_copy(1, j, acc, False)
+                if n == 1:
+                    tanh_of[t - 1]()
             if t >= TILES_HALF:
+                acc = mx_product_tile(t, (6, 7, 8, 9), *MX)
+                mx_copy_tile(t, (6, 7, 8, 9), acc)
+                tanh_of[t - 1]()
                 acc = mx_product_tile(t, (10, 11, 12, 13), *MX)
                 mx_copy_tile(t, (10, 11, 12, 13), acc)
-            if t and not MX_CHUNKS[t]:
+            if 0 < t < 4 and not MX_CHUNKS[t]:
                 tanh_of[t - 1]()
             plain_product(t, 1)
             add_mx(t, 0)
@@ -494,8 +495,11 @@ def tile_share_lstm_cell_pa_kernel(
                 step()
             tanh_of[t] = tanh
         tanh_of[TILES - 1]()
-        left = share_steps(TILES - 1, slice(0, DH // 2), False)
-        right = share_steps(TILES - 1, slice(DH // 2, DH), True)
-        for a, b in zip(left, right):
-            a()
-            b()
+        whole = share_steps(TILES - 1, slice(0, DH), True)
+        halves = [share_steps(TILES - 1, slice(n * P, (n + 1) * P), n == 1) for n in range(2)]
+        s_0, h_t, r_1, p_2 = whole[0], whole[1], whole[2], whole[4]
+        for step in (s_0, h_t, r_1, p_2):
+            step()
+        for n in (3, 5, 6):
+            halves[0][n]()
+            halves[1][n]()

@@ -429,20 +429,20 @@ def tile_share_lstm_cell_pa_kernel(
         SUM, MX, TR = (psum_sum, "sum"), (psum_mx, "mx"), (psum_tr, "tr")
         keep_busy(4)
         transpose_x(0, nc.scalar.copy, *SUM)
-        transpose_x(1, nc.vector.tensor_copy, *SUM)
+        transpose_x(1, nc.scalar.copy, *SUM)
         quantize_x(0)
         quantize_x(1)
+        sum_bias()
         keep_busy(2)
         transpose_x(2, nc.scalar.copy, *MX)
-        sum_bias()
-        transpose_x(3, nc.vector.tensor_copy, *MX)
+        transpose_x(3, nc.scalar.copy, *MX)
         quantize_x(2)
         quantize_x(3)
-        transpose_weights(0, 4, nc.scalar.copy)
+        keep_busy(2)
+        transpose_weights(0, 4, nc.vector.tensor_copy)
         transpose_weights(4, 8, nc.scalar.copy)
         transpose_bias()
         prepare_factors()
-        keep_busy(2)
         for j in range(GATE_TILES):
             acc = mx_product(0, j, *(MX if j % 2 == 0 else SUM))
             mx_copy(0, j, acc, j % 2 == 0 and j < 8)

@@ -29,7 +29,7 @@ K_PASS = 4 * P
 PASSES = DI // K_PASS
 BANK = 512
 
-MX_CHUNKS = ((), (0, 1, 2), (3, 4, 5), (), (), (), (), ())
+MX_CHUNKS = ((), (0, 1, 2), (3, 4, 5), (6, 7), (), (), (), ())
 QUAD = 32
 
 FLOPS = 2 * ROWS * GATES * (DI + DH)
@@ -465,12 +465,12 @@ def tile_share_lstm_cell_pa_kernel(
                 mx_copy(1, j, acc, False)
                 if n == 1:
                     tanh_of[t - 1]()
-            if t >= TILES_HALF:
-                acc = mx_product_tile(t, (6, 7, 8, 9), *MX)
-                mx_copy_tile(t, (6, 7, 8, 9), acc)
+            if t >= 4:
                 tanh_of[t - 1]()
-                acc = mx_product_tile(t, (10, 11, 12, 13), *MX)
-                mx_copy_tile(t, (10, 11, 12, 13), acc)
+            if t >= TILES_HALF:
+                for blocks in ((8, 9, 10, 11), (12, 13)):
+                    acc = mx_product_tile(t, blocks, *MX)
+                    mx_copy_tile(t, blocks, acc)
             if 0 < t < 4 and not MX_CHUNKS[t]:
                 tanh_of[t - 1]()
             plain_product(t, 1)
@@ -487,7 +487,7 @@ def tile_share_lstm_cell_pa_kernel(
             if t + 1 < TILES:
                 plain_product(t + 1, 0)
             kept, new, c_t, tanh, b_o = cell_steps(t)
-            order = [kept, new, b_o, c_t]
+            order = [kept, new, c_t, b_o]
             if t:
                 s_0, h_t, r_1, s_1, p_2, r_2, s_2 = share_steps(t - 1, slice(0, DH), True)
                 order = [s_0, h_t, r_1, kept, p_2, new, s_1, c_t, r_2, b_o, s_2]

from contextlib import ExitStack

import concourse.mybir as mybir
from concourse.masks import make_identity

F32 = mybir.dt.float32
BF16 = mybir.dt.bfloat16
I32 = mybir.dt.int32
U32 = mybir.dt.uint32
U8 = mybir.dt.uint8
FP8X4 = mybir.dt.float8_e4m3fn_x4
FP4X4 = mybir.dt.float4_e2m1fn_x4
ALU = mybir.AluOpType
ACT = mybir.ActivationFunctionType

P = 128
ROWS = 1024
DI = 1024
DH = 256
TILES = ROWS // P
HALVES = 2
TILES_HALF = TILES // HALVES
HALF = ROWS // HALVES
LSTM = 4 * DH
GATES = 7 * DH
GATE_TILES = GATES // P
HALF_BLOCKS = GATE_TILES // 2
K_PASS = 4 * P
PASSES = DI // K_PASS
BANK = 512

MX_CHUNKS = ((), (0, 1, 2), (3, 4, 5), (6, 7), (), (), (), ())
QUAD = 32

FLOPS = 2 * ROWS * GATES * (DI + DH)


def tile_share_lstm_cell_pa_kernel(
    tc,
    x,
    h_minors,
    c_minors,
    s0,
    s1,
    s2,
    mask,
    weight_ih_words,
    weight_ih_scales,
    bias_ih,
    weight_hh,
    bias_hh,
    weight_sh0,
    bias_sh0,
    weight_sh1,
    bias_sh1,
    weight_sh2,
    bias_sh2,
    out_0,
    out_1,
    out_2,
    out_3,
    out_4,
):
    nc = tc.nc
    with ExitStack() as ctx:
        keep = ctx.enter_context(tc.tile_pool(name="keep", bufs=1))
        stage = ctx.enter_context(tc.tile_pool(name="stage", bufs=3))
        chain = ctx.enter_context(tc.tile_pool(name="chain", bufs=3))
        temps = ctx.enter_context(tc.tile_pool(name="temps", bufs=2))
        results = ctx.enter_context(tc.tile_pool(name="results", bufs=3))
        psum_tr = ctx.enter_context(tc.psum_pool(name="psum_tr", bufs=1))
        psum_mx = ctx.enter_context(tc.psum_pool(name="psum_mx", bufs=3))
        psum_sum = ctx.enter_context(tc.psum_pool(name="psum_sum", bufs=4))

        w_scales = keep.tile([P, PASSES, GATES], U8, align_bytes=64)
        nc.vector.memset(w_scales[:].rearrange("p g n -> p (g n)").bitcast(I32), 0)
        bias_x_rows = keep.tile([P, P], BF16)
        nc.vector.memset(bias_x_rows[:], 0.0)
        bias_s_rows = keep.tile([P, P], BF16)
        nc.vector.memset(bias_s_rows[:], 0.0)
        idle_sb = keep.tile([P, BANK], BF16)
        nc.vector.memset(idle_sb[:], 0.0)
        warm_in = keep.tile([P, 1], F32)
        nc.vector.memset(warm_in[:], 0.0)
        warm_out = keep.tile([P, 1], F32)
        nc.scalar.activation(out=warm_out[:], in_=warm_in[:], func=ACT.Sigmoid)

        x_sb = keep.tile([P, TILES_HALF, DI], BF16)
        x_view = x.rearrange("(t p) k -> p t k", p=P)
        states = (h_minors, s0, s1, s2)
        state_views = [s.rearrange("(t p) d -> p t d", p=P) for s in states]
        state_sb = [keep.tile([P, TILES, DH], BF16, name="state_sb%d" % j) for j in range(4)]
        x_quads = keep.tile([P, PASSES, HALF // QUAD, P], BF16, align_bytes=64)

        def load_x(first, last):
            nc.sync.dma_start(out=x_sb[:, first:last, :], in_=x_view[:, first:last, :])

        def load_states(first, last):
            for j in range(4):
                nc.sync.dma_start(out=state_sb[j][:, first:last, :], in_=state_views[j][:, first:last, :])

        def load_x_quads():
            view = x[HALF:ROWS, :].rearrange("(b j) (g r w) -> g r j b w", j=QUAD, g=PASSES, r=4)
            for g in range(PASSES):
                for r in range(4):
                    nc.sync.dma_start(out=x_quads[QUAD * r : QUAD * (r + 1), g, :, :], in_=view[g, r])

        load_x(0, 1)
        load_x(1, 2)
        for quad in range(4):
            nc.sync.dma_start(
                out=w_scales[32 * quad : 32 * quad + 4, :, :].bitcast(I32),
                in_=weight_ih_scales[:, 4 * quad : 4 * quad + 4, :].bitcast(I32).rearrange("g r n -> r g n"),
            )
        load_x(2, 4)
        w_words = keep.tile([P, 2, PASSES, GATES], U8, align_bytes=64)

        def load_words(part):
            some = slice(part * GATES, (part + 1) * GATES)
            nc.sync.dma_start(
                out=w_words[:, part, :, :].bitcast(I32),
                in_=weight_ih_words[:, :, some].bitcast(I32).rearrange("g p n -> p g n"),
            )

        load_words(0)
        nc.sync.dma_start(out=bias_x_rows[0:GATE_TILES, :], in_=bias_ih.rearrange("(j p) -> j p", p=P))
        nc.sync.dma_start(
            out=bias_x_rows[GATE_TILES : GATE_TILES + TILES, :], in_=mask.rearrange("(t p) -> t p", p=P)
        )
        nc.sync.dma_start(out=bias_s_rows[0 : LSTM // P, :], in_=bias_hh.rearrange("(j p) -> j p", p=P))
        for i, bias_sh in enumerate((bias_sh0, bias_sh1, bias_sh2)):
            first = (LSTM + i * DH) // P
            nc.sync.dma_start(out=bias_s_rows[first : first + DH // P, :], in_=bias_sh.rearrange("(j p) -> j p", p=P))
        load_words(1)
        load_states(0, 2)
        load_x_quads()
        load_states(2, 4)
        c_sb = keep.tile([P, TILES, DH], BF16)
        nc.sync.dma_start(out=c_sb[:], in_=c_minors.rearrange("(t p) d -> p t d", p=P))
        load_states(4, TILES)

        ident = keep.tile([P, P], F32)
        make_identity(nc, ident[:])
        whh_sb = keep.tile([P, LSTM // P, DH], BF16)
        nc.gpsimd.dma_start(out=whh_sb[:], in_=weight_hh.rearrange("(j p) k -> p j k", p=P))
        weight_row_tiles = [whh_sb[:, j, :] for j in range(LSTM // P)]
        for i, weight_sh in enumerate((weight_sh0, weight_sh1, weight_sh2)):
            wsh_sb = keep.tile([P, DH // P, DH], BF16, name="wsh_sb%d" % i)
            nc.gpsimd.dma_start(out=wsh_sb[:], in_=weight_sh.rearrange("(j p) k -> p j k", p=P))
            weight_row_tiles.extend([wsh_sb[:, j, :] for j in range(DH // P)])

        bias_rows = keep.tile([P, P], F32)
        columns = keep.tile([P, GATE_TILES + TILES], F32)
        bias_col = columns[:, 0:GATE_TILES]
        factors = keep.tile([P, 3, TILES], F32)

        def sum_bias():
            nc.vector.tensor_tensor(out=bias_rows[:], in0=bias_x_rows[:], in1=bias_s_rows[:], op=ALU.add)

        def transpose_bias():
            bias_ps = psum_tr.tile([P, 4, P], F32, tag="tr")
            nc.tensor.transpose(bias_ps[:, 0, :], bias_rows[:], ident[:])
            nc.vector.tensor_copy(out=columns[:], in_=bias_ps[:, 0, 0 : GATE_TILES + TILES])

        def prepare_factors():
            for n in range(3):
                nc.vector.tensor_scalar(
                    out=factors[:, n, :],
                    in0=columns[:, GATE_TILES : GATE_TILES + TILES],
                    scalar1=1.0 / (n + 1),
                    scalar2=None,
                    op0=ALU.mult,
                )

        w_t = keep.tile([P, GATES], F32)
        w_t_halves = w_t[:].bitcast(BF16).rearrange("p (n e) -> p n e", e=2)

        def transpose_weights(first, last, copy):
            group = weight_row_tiles[first:last]
            wt_ps = psum_sum.tile([P, 4, P], F32, tag="sum")
            for j, rows in enumerate(group):
                nc.tensor.transpose(wt_ps[:, j, :], rows.bitcast(F32), ident[:])
            copy(
                out=w_t[:, first * P : last * P],
                in_=wt_ps[:, 0 : len(group), :].rearrange("p j n -> p (j n)"),
            )

        x_codes = keep.tile([P, HALVES, PASSES, HALF], U32, align_bytes=64)
        x_scales = keep.tile([P, HALVES, PASSES, HALF], U8, align_bytes=64)
        states_t_sb = keep.tile([P, TILES, 4, P], F32)
        mx_sb = keep.tile([P, HALVES, GATE_TILES, HALF], F32)
        gates = {}
        grouped_x = {}

        def transpose_x(t, copy, pool, tag):
            x_words = x_sb[:, t, :].bitcast(F32)
            xt_ps = pool.tile([P, PASSES, 2, P], F32, tag=tag)
            for g in range(PASSES):
                for u in range(2):
                    nc.tensor.transpose(
                        xt_ps[:, g, u, :], x_words[:, (K_PASS // 2) * g + u : (K_PASS // 2) * (g + 1) : 2], ident[:]
                    )
            grouped = stage.tile([P, PASSES, P, 4], BF16, align_bytes=64)
            copy(out=grouped[:].bitcast(F32), in_=xt_ps[:].rearrange("p g u r -> p g r u"))
            grouped_x[t] = grouped

        def quantize_x(t):
            for g in range(PASSES):
                nc.vector.quantize_mx(
                    out=x_codes[:, 0, g, t * P : (t + 1) * P].bitcast(FP8X4),
                    scales=x_scales[:, 0, g, t * P : (t + 1) * P],
                    in_=grouped_x[t][:, g, :, :].rearrange("p r k -> p (r k)"),
                )

        def split_x_quads(g, copy):
            parted = stage.tile([P, 2, HALF // QUAD, QUAD], F32, align_bytes=64)
            copy(
                out=parted[:],
                in_=x_quads[:, g, :, :].bitcast(F32).rearrange("p b (i u) -> p u b i", u=2),
            )
            return parted

        def turn_x_quads(parted):
            turned = stage.tile([P, 2, HALF], F32, align_bytes=64)
            nc.vector.transpose(turned[:].rearrange("p u r -> p (u r)"), parted[:].rearrange("p u b i -> p (u b i)"))
            return turned

        def group_x_quads(turned, copy):
            grouped = stage.tile([P, HALF, 4], BF16, align_bytes=64)
            copy(out=grouped[:].rearrange("p r k -> p (r k)").bitcast(F32).rearrange("p (r u) -> p r u", u=2), in_=turned[:].rearrange("p u r -> p r u"))
            return grouped

        def quantize_x_quads(g, grouped):
            nc.vector.quantize_mx(
                out=x_codes[:, 1, g, :].bitcast(FP8X4),
                scales=x_scales[:, 1, g, :],
                in_=grouped[:].rearrange("p r k -> p (r k)"),
            )

        def transpose_states(t, copy, pool, tag):
            st_ps = pool.tile([P, 4, P], F32, tag=tag)
            for j in range(4):
                nc.tensor.transpose(st_ps[:, j, :], state_sb[j][:, t, :].bitcast(F32), ident[:])
            copy(out=states_t_sb[:, t, :, :], in_=st_ps[:])

        def mx_product(half, j, pool, tag):
            acc = pool.tile([P, HALF], F32, tag=tag)
            for g in range(PASSES):
                nc.tensor.matmul_mx(
                    out=acc[:],
                    lhsT=w_words[:, j // HALF_BLOCKS, g, 2 * P * (j % HALF_BLOCKS) : 2 * P * (j % HALF_BLOCKS + 1)].bitcast(
                        FP4X4
                    ),
                    lhsT_scale=w_scales[:, g, P * j : P * (j + 1)],
                    rhs=x_codes[:, half, g, :].bitcast(FP8X4),
                    rhs_scale=x_scales[:, half, g, :],
                    start=(g == 0),
                    stop=(g == PASSES - 1),
                )
            return acc

        def mx_product_tile(t, blocks, pool, tag):
            half, place = divmod(t, TILES_HALF)
            rows = slice(place * P, (place + 1) * P)
            acc = pool.tile([P, BANK // P, P], F32, tag=tag)
            for n, j in enumerate(blocks):
                for g in range(PASSES):
                    nc.tensor.matmul_mx(
                        out=acc[:, n, :],
                        lhsT=w_words[:, j // HALF_BLOCKS, g, 2 * P * (j % HALF_BLOCKS) : 2 * P * (j % HALF_BLOCKS + 1)].bitcast(
                            FP4X4
                        ),
                        lhsT_scale=w_scales[:, g, P * j : P * (j + 1)],
                        rhs=x_codes[:, half, g, rows].bitcast(FP8X4),
                        rhs_scale=x_scales[:, half, g, rows],
                        start=(g == 0),
                        stop=(g == PASSES - 1),
                    )
            return acc

        def mx_copy_tile(t, blocks, acc):
            half, place = divmod(t, TILES_HALF)
            rows = slice(place * P, (place + 1) * P)
            for n, j in enumerate(blocks):
                nc.scalar.activation(
                    out=mx_sb[:, half, j, rows], in_=acc[:, n, :], func=ACT.Identity, bias=bias_col[:, j : j + 1]
                )

        def mx_copy(half, j, acc, on_vector):
            if on_vector:
                nc.vector.tensor_scalar(
                    out=mx_sb[:, half, j, :], in0=acc[:], scalar1=bias_col[:, j : j + 1], scalar2=None, op0=ALU.add
                )
            else:
                nc.scalar.activation(out=mx_sb[:, half, j, :], in_=acc[:], func=ACT.Identity, bias=bias_col[:, j : j + 1])

        sums = {}

        def plain_product(t, bank):
            states_t = states_t_sb[:, t, :, :].bitcast(BF16).rearrange("p j (r e) -> p j r e", e=2)
            c0 = bank * BANK
            width = min(BANK, GATES - c0)
            total = psum_sum.tile([P, BANK], F32, tag="sum")
            sums[t, bank] = total
            step = BANK if c0 < LSTM else DH
            for b0 in range(c0, c0 + width, step):
                source = max(0, b0 // DH - 3)
                for e in range(2):
                    nc.tensor.matmul(
                        total[:, b0 - c0 : b0 - c0 + step],
                        lhsT=states_t[:, source, :, e],
                        rhs=w_t_halves[:, b0 : b0 + step, e],
                        start=(b0 == c0 and e == 0),
                        stop=False,
                    )

        def add_mx(t, bank):
            half, place = divmod(t, TILES_HALF)
            c0 = bank * BANK
            blocks = range(c0 // P, min(c0 + BANK, GATES) // P)
            for j in blocks:
                nc.tensor.matmul(
                    sums[t, bank][:, j * P - c0 : (j + 1) * P - c0],
                    lhsT=mx_sb[:, half, j, place * P : (place + 1) * P],
                    rhs=ident[:],
                    is_transpose=True,
                    start=False,
                    stop=(j == blocks[-1]),
                )

        def activate(t, banks):
            if 0 in banks:
                gates[t] = chain.tile([P, GATES], F32, name="gate")
            gate = gates[t]
            for bank in banks:
                c0 = bank * BANK
                width = min(BANK, GATES - c0)
                total = sums[t, bank]
                if c0 == 2 * DH:
                    nc.scalar.activation(out=gate[:, c0 : c0 + DH], in_=total[:, 0:DH], func=ACT.Sigmoid)
                    nc.scalar.activation(out=gate[:, c0 + DH : c0 + BANK], in_=total[:, DH:BANK], func=ACT.Tanh)
                else:
                    nc.scalar.activation(out=gate[:, c0 : c0 + width], in_=total[:, 0:width], func=ACT.Sigmoid)

        out_views = [o.rearrange("(t p) d -> p t d", p=P) for o in (out_0, out_1, out_2, out_3, out_4)]

        def fused(out, in0, scalar, in1, op0, op1):
            nc.vector.scalar_tensor_tensor(out=out, in0=in0, scalar=scalar, in1=in1, op0=op0, op1=op1)

        work = {}

        def cell_steps(t):
            gate = gates[t]
            m = factors[:, 0, t : t + 1]
            res = results.tile([P, 5, DH], F32)
            kept = temps.tile([P, DH], F32)
            new = temps.tile([P, DH], F32)
            tanh_c = temps.tile([P, DH], F32)
            b_o = temps.tile([P, 3, DH], F32)
            rests = [temps.tile([P, DH], F32, name="rest%d" % n) for n in range(3)]
            work[t] = (res, tanh_c, b_o, rests)
            o_g = gate[:, 2 * DH : 3 * DH]
            b_g = gate[:, LSTM:GATES].rearrange("p (j d) -> p j d", j=3)

            def step_kept():
                fused(kept[:], gate[:, DH : 2 * DH], m, c_sb[:, t, :], ALU.mult, ALU.mult)

            def step_new():
                fused(new[:], gate[:, 0:DH], m, gate[:, 3 * DH : LSTM], ALU.mult, ALU.mult)

            def step_c():
                nc.vector.tensor_tensor(out=res[:, 1, :], in0=kept[:], in1=new[:], op=ALU.add)

            def step_tanh():
                nc.scalar.activation(out=tanh_c[:], in_=res[:, 1, :], func=ACT.Tanh)
                nc.sync.dma_start(out=out_views[1][:, t, :], in_=res[:, 1, :])

            def step_b():
                fused(b_o[:], b_g, 1.0, o_g.unsqueeze(1).to_broadcast([P, 3, DH]), ALU.add, ALU.subtract)

            return step_kept, step_new, step_c, step_tanh, step_b

        def share_steps(t, cols, stores):
            res, tanh_c_all, b_o, (rest1, part2, rest2) = work[t]
            tanh_c = tanh_c_all[:, cols]
            m1, m2, m3 = [factors[:, n, t : t + 1] for n in range(3)]
            o_g = gates[t][:, 2 * DH + cols.start : 2 * DH + cols.stop]

            def store(k):
                if stores:
                    nc.sync.dma_start(out=out_views[k][:, t, :], in_=res[:, k, :])

            def step_s0():
                fused(res[:, 2, cols], b_o[:, 0, cols], m1, tanh_c, ALU.mult, ALU.mult)
                store(2)

            def step_rest1():
                fused(rest1[:, cols], b_o[:, 1, cols], 1.0, res[:, 2, cols], ALU.add, ALU.subtract)

            def step_s1():
                fused(res[:, 3, cols], rest1[:, cols], m2, tanh_c, ALU.mult, ALU.mult)
                store(3)

            def step_part2():
                fused(part2[:, cols], res[:, 2, cols], -2.0, b_o[:, 2, cols], ALU.mult, ALU.add)

            def step_rest2():
                fused(rest2[:, cols], part2[:, cols], 2.0, res[:, 3, cols], ALU.add, ALU.subtract)

            def step_s2():
                fused(res[:, 4, cols], rest2[:, cols], m3, tanh_c, ALU.mult, ALU.mult)
                store(4)

            def step_h():
                fused(res[:, 0, cols], o_g, m1, tanh_c, ALU.mult, ALU.mult)
                store(0)

            return step_s0, step_h, step_rest1, step_s1, step_part2, step_rest2, step_s2

        ctx.enter_context(
            tc.manual_schedule(engines={mybir.EngineType.PE, mybir.EngineType.Activation, mybir.EngineType.DVE})
        )
        idle_ps = psum_mx.tile([P, BANK], F32, tag="mx")

        def keep_busy(times):
            for i in range(times):
                nc.tensor.matmul(idle_ps[:], lhsT=idle_sb[:, 0:P], rhs=idle_sb[:], start=True, stop=True)

        SUM, MX, TR = (psum_sum, "sum"), (psum_mx, "mx"), (psum_tr, "tr")
        keep_busy(4)
        transpose_x(0, nc.scalar.copy, *SUM)
        transpose_x(1, nc.scalar.copy, *SUM)
        quantize_x(0)
        quantize_x(1)
        sum_bias()
        keep_busy(2)
        transpose_x(2, nc.scalar.copy, *MX)
        transpose_x(3, nc.scalar.copy, *MX)
        quantize_x(2)
        quantize_x(3)
        keep_busy(2)
        transpose_weights(0, 4, nc.vector.tensor_copy)
        transpose_weights(4, 8, nc.scalar.copy)
        transpose_bias()
        prepare_factors()
        for j in range(GATE_TILES):
            acc = mx_product(0, j, *(MX if j % 2 == 0 else SUM))
            mx_copy(0, j, acc, j % 2 == 0 and j < 8)
        transpose_states(0, nc.scalar.copy, *MX)
        transpose_weights(8, 12, nc.scalar.copy)
        transpose_weights(12, 14, nc.scalar.copy)
        transpose_states(1, nc.scalar.copy, *MX)
        transpose_states(2, nc.scalar.copy, *MX)
        transpose_states(3, nc.scalar.copy, *TR)
        parted = [split_x_quads(g, nc.vector.tensor_copy) for g in range(PASSES)]
        turned = [turn_x_quads(p) for p in parted]
        grouped = [group_x_quads(p, nc.vector.tensor_copy) for p in turned]
        for g in range(PASSES):
            quantize_x_quads(g, grouped[g])
        plain_product(0, 0)
        tanh_of = {}
        for t in range(TILES):
            for n, j in enumerate(MX_CHUNKS[t]):
                acc = mx_product(1, j, *MX)
                mx_copy(1, j, acc, False)
                if n == 1:
                    tanh_of[t - 1]()
            if t >= 4:
                tanh_of[t - 1]()
            if t >= TILES_HALF:
                for blocks in ((8, 9, 10, 11), (12, 13)):
                    acc = mx_product_tile(t, blocks, *MX)
                    mx_copy_tile(t, blocks, acc)
            if 0 < t < 4 and not MX_CHUNKS[t]:
                tanh_of[t - 1]()
            plain_product(t, 1)
            add_mx(t, 0)
            add_mx(t, 1)
            activate(t, (0, 1))
            plain_product(t, 2)
            plain_product(t, 3)
            add_mx(t, 2)
            add_mx(t, 3)
            activate(t, (2, 3))
            if 2 <= t < TILES_HALF + 2:
                transpose_states(t + 2, nc.scalar.copy, *TR)
            if t + 1 < TILES:
                plain_product(t + 1, 0)
            kept, new, c_t, tanh, b_o = cell_steps(t)
            order = [kept, new, c_t, b_o]
            if t:
                s_0, h_t, r_1, s_1, p_2, r_2, s_2 = share_steps(t - 1, slice(0, DH), True)
                order = [s_0, h_t, r_1, kept, p_2, new, s_1, c_t, r_2, b_o, s_2]
            for step in order:
                step()
            tanh_of[t] = tanh
        tanh_of[TILES - 1]()
        whole = share_steps(TILES - 1, slice(0, DH), True)
        halves = [share_steps(TILES - 1, slice(n * P, (n + 1) * P), n == 1) for n in range(2)]
        s_0, h_t, r_1, p_2 = whole[0], whole[1], whole[2], whole[4]
        for step in (s_0, h_t, r_1, p_2):
            step()
        for n in (3, 5, 6):
            halves[0][n]()
            halves[1][n]()
